import numpy as np
import ml_dtypes


def mxq(x, axis, fmt="e4m3"):
    dtype, down = {"e4m3": (ml_dtypes.float8_e4m3fn, 7), "e5m2": (ml_dtypes.float8_e5m2, 14)}[fmt]
    v = np.moveaxis(np.asarray(x, np.float32).astype(ml_dtypes.bfloat16).astype(np.float64), axis, -1)
    blocks = v.reshape(v.shape[:-1] + (-1, 32))
    amax = np.abs(blocks).max(-1, keepdims=True)
    byte = np.maximum(np.where(amax > 0, np.frexp(amax)[1] - 1 + 127, 0) - down, 1)
    scale = np.exp2(byte - 127.0)
    codes = (blocks / scale).astype(np.float32).astype(dtype).astype(np.float64)
    return np.moveaxis((codes * scale).reshape(v.shape), -1, axis)


WIDE = False


def mx_kscale(k):
    if not WIDE:
        return np.ones(k)
    levels = np.array([10, -10, 5, -5, 0])
    a = np.random.permutation(np.resize(levels, k // 512 * 4)).reshape(k // 512, 4)
    idx = np.arange(k)
    return np.exp2(a[idx // 512, idx % 128 // 32])


BF16 = ml_dtypes.bfloat16


def bf(x):
    return np.asarray(x, np.float32).astype(BF16)


def f64(x):
    return np.asarray(x).astype(np.float64)


B, I, H = 1024, 1024, 1024
EPS = 1e-5


def ln(v):
    mu = v.mean(-1, keepdims=True)
    var = np.square(v - mu).mean(-1, keepdims=True)
    return (v - mu) / np.sqrt(var + EPS)


def sigmoid(v):
    return 1.0 / (1.0 + np.exp(-v))


def setup_inputs():
    s = mx_kscale(I)
    return {"x": bf(np.random.standard_normal((B, I)) * s),
            "h": bf(np.random.standard_normal((B, H))),
            "r": bf(sigmoid(np.sqrt(2.0) * np.random.standard_normal((B, H)))),
            "z": bf(sigmoid(np.sqrt(2.0) * np.random.standard_normal((B, H)))),
            "W_in": bf(np.random.standard_normal((H, I)) / np.sqrt(I) / s),
            "b_in": bf(np.random.standard_normal(H) * 0.5),
            "W_hn": bf(np.random.standard_normal((H, H)) / np.sqrt(H)),
            "b_hn": bf(np.random.standard_normal(H) * 0.5)}


def reference(x, h, r, z, W_in, b_in, W_hn, b_hn):
    h = f64(h)
    r, z = f64(r), f64(z)
    i_n = ln((mxq(f64(x), 1, "e4m3") @ mxq(f64(W_in), 1, "e4m3").T) + f64(b_in))
    h_n = ln((mxq(h, 1, "e4m3") @ mxq(f64(W_hn), 1, "e4m3").T) + f64(b_hn))
    n = np.tanh(i_n + r * h_n)
    return (1.0 - z) * n + z * h

@@ -1,0 +1,202 @@
+from contextlib import ExitStack
+
+import concourse.mybir as mybir
+from concourse.masks import make_identity
+
+F32 = mybir.dt.float32
+BF16 = mybir.dt.bfloat16
+U32 = mybir.dt.uint32
+U8 = mybir.dt.uint8
+I32 = mybir.dt.int32
+FP8X4 = mybir.dt.float8_e4m3fn_x4
+ALU = mybir.AluOpType
+ACT = mybir.ActivationFunctionType
+
+P = 128
+N = 1024
+NT = N // P
+HALF = 512
+EPS = 1e-5
+FLOPS = 2 * 2 * N * N * N
+PIN = False
+
+
+def tile_layernormgrucell_pb_kernel(tc, x, h, r, z, W_in, b_in, W_hn, b_hn, out):
+    nc = tc.nc
+    with ExitStack() as ctx:
+        if PIN:
+            ctx.enter_context(tc.manual_schedule())
+        const = ctx.enter_context(tc.tile_pool(name="const", bufs=1))
+        rawp = ctx.enter_context(tc.tile_pool(name="raw", bufs=4))
+        grp = ctx.enter_context(tc.tile_pool(name="grouped", bufs=2))
+        keep = ctx.enter_context(tc.tile_pool(name="keep", bufs=1))
+        tpp = ctx.enter_context(tc.psum_pool(name="tp", bufs=4))
+        mxp = ctx.enter_context(tc.psum_pool(name="mx", bufs=4))
+
+        ident = const.tile([P, P], F32, name="ident")
+        make_identity(nc, ident[:])
+        ones = const.tile([P, P], BF16, name="ones")
+        nc.vector.memset(ones[:], 1.0)
+        zb = const.tile([P, 2 * N], BF16, name="zb")
+        nc.vector.memset(zb[:].bitcast(I32), 0)
+        eps_t = const.tile([P, 1], F32, name="eps_t")
+        nc.vector.memset(eps_t[:], EPS)
+        scr = const.tile([P, 2], F32, name="scr")
+        nc.scalar.activation(out=scr[:, 0:1], in_=eps_t[:], func=ACT.Sqrt)
+        nc.scalar.dma_start(out=zb[0:1, 0:N], in_=b_in.rearrange("(o n) -> o n", o=1))
+        nc.scalar.dma_start(out=zb[0:1, N:2 * N], in_=b_hn.rearrange("(o n) -> o n", o=1))
+
+        bias = const.tile([P, 2 * N], F32, name="bias")
+        sums = const.tile([P, 4 * NT], F32, name="sums")
+        nmu = const.tile([P, 2 * NT], F32, name="nmu")
+        ssq = const.tile([P, 2 * NT], F32, name="ssq")
+        std = const.tile([P, 2 * NT], F32, name="std")
+        rho = const.tile([P, 2 * NT], F32, name="rho")
+        kap = const.tile([P, NT], F32, name="kap")
+        nb = const.tile([P, NT], F32, name="nb")
+        junk = const.tile([P, N], F32, name="junk")
+
+        w_views = [W_in.rearrange("(c p) k -> p c k", p=P), W_hn.rearrange("(c p) k -> p c k", p=P)]
+        x_v = x.rearrange("(p t) k -> p t k", t=NT)
+        h_v = h.rearrange("(p t) k -> p t k", t=NT)
+        r_v = r.rearrange("(p t) k -> p t k", t=NT)
+        z_v = z.rearrange("(p t) k -> p t k", t=NT)
+        out_v = out.rearrange("(p t) k -> p t k", t=NT)
+
+        def load_pairs(view, tag, resident):
+            tiles = []
+            for i in range(NT // 2):
+                if resident:
+                    t_ = keep.tile([P, 2 * N], BF16, name="%s%d" % (tag, i))
+                else:
+                    t_ = rawp.tile([P, 2 * N], BF16, name="%s%d" % (tag, i), tag=tag[0:2])
+                nc.sync.dma_start(out=t_[:].rearrange("p (c k) -> p c k", c=2),
+                                  in_=view[:, 2 * i:2 * i + 2, :])
+                tiles.append(t_)
+            return tiles
+
+        win_raw = load_pairs(w_views[0], "wwin", False)
+        x_raw = load_pairs(x_v, "xrx", False)
+        whn_raw = load_pairs(w_views[1], "wwhn", False)
+        h_raw = load_pairs(h_v, "hraw", True)
+        r_raw = load_pairs(r_v, "xrr", False)
+        z_raw = load_pairs(z_v, "zraw", True)
+
+        for k in range(4):
+            ps = mxp.tile([P, HALF], F32, name="ps", tag="mx")
+            nc.tensor.matmul(out=ps[:], lhsT=ones[:], rhs=zb[:, k * HALF:(k + 1) * HALF],
+                             start=True, stop=True)
+            nc.vector.tensor_copy(out=bias[:, k * HALF:(k + 1) * HALF], in_=ps[:])
+
+        def transpose_block(raw_pair, cc):
+            tp = tpp.tile([P, HALF], F32, name="tp", tag="tp")
+            words = raw_pair[:].bitcast(F32)
+            for q in range(4):
+                nc.tensor.transpose(tp[:, q * P:(q + 1) * P],
+                                    words[:, cc * HALF + q * P:cc * HALF + (q + 1) * P], ident[:])
+            return tp
+
+        def evacuate(on_vector, tp, dst):
+            src = tp[:].rearrange("p (g u r) -> p g r u", g=2, u=2)
+            if on_vector:
+                nc.vector.tensor_copy(out=dst, in_=src)
+            else:
+                nc.scalar.copy(out=dst, in_=src)
+
+        def prepare_weight(raw, name, vector_chunks):
+            codes = keep.tile([P, 2 * N], U32, name="c" + name, align_bytes=64)
+            scales = keep.tile([P, 2 * N], U8, name="s" + name, align_bytes=64)
+            for half in range(2):
+                gw = grp.tile([P, 4 * N], BF16, name="gw", tag="gw", align_bytes=64)
+                gview = gw[:].bitcast(F32).rearrange("p (g c r u) -> p g c r u", g=2, c=4, u=2)
+                for c4 in range(4):
+                    c = 4 * half + c4
+                    tp = transpose_block(raw[c // 2], c % 2)
+                    evacuate(c in vector_chunks, tp, gview[:, :, c4, :, :])
+                for g in range(2):
+                    cols = slice(g * N + half * HALF, g * N + (half + 1) * HALF)
+                    nc.vector.quantize_mx(out=codes[:, cols].bitcast(FP8X4), scales=scales[:, cols],
+                                          in_=gw[:, g * 2 * N:(g + 1) * 2 * N])
+            return codes, scales
+
+        def prepare_rows(raw, t, codes, scales):
+            tp = transpose_block(raw[t // 2], t % 2)
+            gx = grp.tile([P, N], BF16, name="gx", tag="gx", bufs=3, align_bytes=64)
+            evacuate(False, tp, gx[:].bitcast(F32).rearrange("p (g r u) -> p g r u", g=2, u=2))
+            cols = slice(t * 2 * P, (t + 1) * 2 * P)
+            nc.vector.quantize_mx(out=codes[:, cols].bitcast(FP8X4), scales=scales[:, cols], in_=gx[:])
+
+        def product_plus_bias(m, t, rows, weight, dst):
+            rc, rs = rows
+            wc, ws = weight
+            for half in range(2):
+                ps = mxp.tile([P, HALF], F32, name="ps", tag="mx")
+                for g in range(2):
+                    lcols = slice(t * 2 * P + g * P, t * 2 * P + (g + 1) * P)
+                    rcols = slice(g * N + half * HALF, g * N + (half + 1) * HALF)
+                    nc.tensor.matmul_mx(out=ps[:], lhsT=rc[:, lcols].bitcast(FP8X4), lhsT_scale=rs[:, lcols],
+                                        rhs=wc[:, rcols].bitcast(FP8X4), rhs_scale=ws[:, rcols],
+                                        start=(g == 0), stop=(g == 1))
+                k = (m * NT + t) * 2 + half
+                nc.vector.scalar_tensor_tensor(
+                    out=dst[:, half * HALF:(half + 1) * HALF], in0=ps[:], scalar=1.0,
+                    in1=bias[:, m * N + half * HALF:m * N + (half + 1) * HALF],
+                    op0=ALU.mult, op1=ALU.add, accum_out=sums[:, k:k + 1])
+
+        def deviation_squares(m, t, src):
+            i = m * NT + t
+            nc.scalar.activation(out=scr[:, 0:2], in_=sums[:, 2 * i:2 * i + 2], func=ACT.Identity,
+                                 scale=-1.0 / N, accum_out=nmu[:, i:i + 1])
+            nc.scalar.activation(out=junk[:], in_=src[:], func=ACT.Square, bias=nmu[:, i:i + 1],
+                                 scale=1.0, accum_out=ssq[:, i:i + 1])
+
+        a_t = [keep.tile([P, N], F32, name="a%d" % t) for t in range(NT)]
+        c_t = [keep.tile([P, N], F32, name="c%d" % t) for t in range(NT)]
+        xq = (keep.tile([P, 2 * N], U32, name="cx", align_bytes=64),
+              keep.tile([P, 2 * N], U8, name="sx", align_bytes=64))
+        hq = (keep.tile([P, 2 * N], U32, name="ch", align_bytes=64),
+              keep.tile([P, 2 * N], U8, name="sh", align_bytes=64))
+
+        win_q = prepare_weight(win_raw, "win", (0, 2, 4, 6))
+        for t in range(NT):
+            prepare_rows(x_raw, t, xq[0], xq[1])
+            product_plus_bias(0, t, xq, win_q, a_t[t])
+            deviation_squares(0, t, a_t[t])
+        whn_q = prepare_weight(whn_raw, "whn", ())
+        for t in range(NT):
+            prepare_rows(h_raw, t, hq[0], hq[1])
+        for t in range(NT):
+            product_plus_bias(1, t, hq, whn_q, c_t[t])
+            deviation_squares(1, t, c_t[t])
+
+        def tile_of(raw, t):
+            return raw[t // 2][:, (t % 2) * N:(t % 2 + 1) * N]
+
+        for t in range(NT):
+            nc.vector.scalar_tensor_tensor(out=c_t[t][:], in0=c_t[t][:], scalar=nmu[:, NT + t:NT + t + 1],
+                                           in1=tile_of(r_raw, t), op0=ALU.add, op1=ALU.mult)
+
+        nc.scalar.activation(out=std[:], in_=ssq[:], func=ACT.Sqrt, bias=eps_t[:], scale=1.0 / N)
+        nc.scalar.activation(out=scr[:, 0:1], in_=eps_t[:], func=ACT.Tanh)
+        nc.vector.reciprocal(out=rho[:], in_=std[:])
+        nc.vector.tensor_tensor(out=kap[:], in0=rho[:, NT:2 * NT], in1=std[:, 0:NT], op=ALU.mult)
+        nc.vector.tensor_tensor(out=nb[:], in0=nmu[:, 0:NT], in1=rho[:, 0:NT], op=ALU.mult)
+
+        def candidate(t):
+            nc.vector.scalar_tensor_tensor(out=a_t[t][:], in0=c_t[t][:], scalar=kap[:, t:t + 1],
+                                           in1=a_t[t][:], op0=ALU.mult, op1=ALU.add)
+            nc.scalar.activation(out=a_t[t][:], in_=a_t[t][:], func=ACT.Tanh,
+                                 bias=nb[:, t:t + 1], scale=rho[:, t:t + 1])
+            nc.vector.tensor_tensor(out=c_t[t][:], in0=tile_of(z_raw, t), in1=tile_of(h_raw, t), op=ALU.mult)
+
+        def blend(t):
+            nc.vector.scalar_tensor_tensor(out=a_t[t][:], in0=tile_of(z_raw, t), scalar=1.0,
+                                           in1=a_t[t][:], op0=ALU.subtract, op1=ALU.mult)
+            nc.vector.tensor_tensor(out=a_t[t][:], in0=c_t[t][:], in1=a_t[t][:], op=ALU.subtract)
+            nc.sync.dma_start(out=out_v[:, t, :], in_=a_t[t][:])
+
+        candidate(0)
+        for t in range(1, NT):
+            candidate(t)
+            blend(t - 1)
+        blend(NT - 1)

@@ -19,6 +19,7 @@ HALF = 512
 EPS = 1e-5
 FLOPS = 2 * 2 * N * N * N
 PIN = False
+NB = 4
 
 
 def tile_layernormgrucell_pb_kernel(tc, x, h, r, z, W_in, b_in, W_hn, b_hn, out):
@@ -33,18 +34,18 @@ def tile_layernormgrucell_pb_kernel(tc, x, h, r, z, W_in, b_in, W_hn, b_hn, out)
         tpp = ctx.enter_context(tc.psum_pool(name="tp", bufs=4))
         mxp = ctx.enter_context(tc.psum_pool(name="mx", bufs=4))
 
+        zb = const.tile([P, 2 * N], BF16, name="zb")
+        nc.vector.memset(zb[:].bitcast(I32), 0)
         ident = const.tile([P, P], F32, name="ident")
         make_identity(nc, ident[:])
         ones = const.tile([P, P], BF16, name="ones")
         nc.vector.memset(ones[:], 1.0)
-        zb = const.tile([P, 2 * N], BF16, name="zb")
-        nc.vector.memset(zb[:].bitcast(I32), 0)
         eps_t = const.tile([P, 1], F32, name="eps_t")
         nc.vector.memset(eps_t[:], EPS)
         scr = const.tile([P, 2], F32, name="scr")
         nc.scalar.activation(out=scr[:, 0:1], in_=eps_t[:], func=ACT.Sqrt)
-        nc.scalar.dma_start(out=zb[0:1, 0:N], in_=b_in.rearrange("(o n) -> o n", o=1))
-        nc.scalar.dma_start(out=zb[0:1, N:2 * N], in_=b_hn.rearrange("(o n) -> o n", o=1))
+        nc.sync.dma_start(out=zb[0:1, 0:N], in_=b_in.rearrange("(o n) -> o n", o=1))
+        nc.sync.dma_start(out=zb[0:1, N:2 * N], in_=b_hn.rearrange("(o n) -> o n", o=1))
 
         bias = const.tile([P, 2 * N], F32, name="bias")
         sums = const.tile([P, 4 * NT], F32, name="sums")
@@ -54,7 +55,7 @@ def tile_layernormgrucell_pb_kernel(tc, x, h, r, z, W_in, b_in, W_hn, b_hn, out)
         rho = const.tile([P, 2 * NT], F32, name="rho")
         kap = const.tile([P, NT], F32, name="kap")
         nb = const.tile([P, NT], F32, name="nb")
-        junk = const.tile([P, N], F32, name="junk")
+        junk = const.tile([P, N], BF16, name="junk")
 
         w_views = [W_in.rearrange("(c p) k -> p c k", p=P), W_hn.rearrange("(c p) k -> p c k", p=P)]
         x_v = x.rearrange("(p t) k -> p t k", t=NT)
@@ -79,14 +80,33 @@ def tile_layernormgrucell_pb_kernel(tc, x, h, r, z, W_in, b_in, W_hn, b_hn, out)
         x_raw = load_pairs(x_v, "xrx", False)
         whn_raw = load_pairs(w_views[1], "wwhn", False)
         h_raw = load_pairs(h_v, "hraw", True)
-        r_raw = load_pairs(r_v, "xrr", False)
         z_raw = load_pairs(z_v, "zraw", True)
+        r_raw = load_pairs(r_v, "xrr", False)
 
-        for k in range(4):
-            ps = mxp.tile([P, HALF], F32, name="ps", tag="mx")
-            nc.tensor.matmul(out=ps[:], lhsT=ones[:], rhs=zb[:, k * HALF:(k + 1) * HALF],
-                             start=True, stop=True)
-            nc.vector.tensor_copy(out=bias[:, k * HALF:(k + 1) * HALF], in_=ps[:])
+        def tile_of(raw, t):
+            return raw[t // 2][:, (t % 2) * N:(t % 2 + 1) * N]
+
+        zh_t = []
+        for t in range(NT):
+            if t < NT // 2:
+                zh = keep.tile([P, N], F32, name="zh%d" % t)
+            else:
+                zh = rawp.tile([P, N], F32, name="zh%d" % t, tag="ww")
+            for i in range(2):
+                cols = slice(i * HALF, (i + 1) * HALF)
+                nc.gpsimd.tensor_tensor(out=zh[:, cols], in0=tile_of(z_raw, t)[:, cols],
+                                        in1=tile_of(h_raw, t)[:, cols], op=ALU.mult)
+            zh_t.append(zh)
+
+        def spread_biases():
+            for k in range(4):
+                ps = mxp.tile([P, HALF], F32, name="ps", tag="mx")
+                nc.tensor.matmul(out=ps[:], lhsT=ones[:], rhs=zb[:, k * HALF:(k + 1) * HALF],
+                                 start=True, stop=True)
+                if k % 2 == 0:
+                    nc.vector.tensor_copy(out=bias[:, k * HALF:(k + 1) * HALF], in_=ps[:])
+                else:
+                    nc.scalar.copy(out=bias[:, k * HALF:(k + 1) * HALF], in_=ps[:])
 
         def transpose_block(raw_pair, cc):
             tp = tpp.tile([P, HALF], F32, name="tp", tag="tp")
@@ -121,7 +141,7 @@ def tile_layernormgrucell_pb_kernel(tc, x, h, r, z, W_in, b_in, W_hn, b_hn, out)
 
         def prepare_rows(raw, t, codes, scales):
             tp = transpose_block(raw[t // 2], t % 2)
-            gx = grp.tile([P, N], BF16, name="gx", tag="gx", bufs=3, align_bytes=64)
+            gx = grp.tile([P, N], BF16, name="gx", tag="gx", bufs=2, align_bytes=64)
             evacuate(False, tp, gx[:].bitcast(F32).rearrange("p (g r u) -> p g r u", g=2, u=2))
             cols = slice(t * 2 * P, (t + 1) * 2 * P)
             nc.vector.quantize_mx(out=codes[:, cols].bitcast(FP8X4), scales=scales[:, cols], in_=gx[:])
@@ -143,12 +163,19 @@ def tile_layernormgrucell_pb_kernel(tc, x, h, r, z, W_in, b_in, W_hn, b_hn, out)
                     in1=bias[:, m * N + half * HALF:m * N + (half + 1) * HALF],
                     op0=ALU.mult, op1=ALU.add, accum_out=sums[:, k:k + 1])
 
-        def deviation_squares(m, t, src):
+        def mean_of(m, t):
             i = m * NT + t
             nc.scalar.activation(out=scr[:, 0:2], in_=sums[:, 2 * i:2 * i + 2], func=ACT.Identity,
                                  scale=-1.0 / N, accum_out=nmu[:, i:i + 1])
+
+        def squares_of(m, t, src):
+            i = m * NT + t
             nc.scalar.activation(out=junk[:], in_=src[:], func=ACT.Square, bias=nmu[:, i:i + 1],
                                  scale=1.0, accum_out=ssq[:, i:i + 1])
+
+        def deviation_squares(m, t, src):
+            mean_of(m, t)
+            squares_of(m, t, src)
 
         a_t = [keep.tile([P, N], F32, name="a%d" % t) for t in range(NT)]
         c_t = [keep.tile([P, N], F32, name="c%d" % t) for t in range(NT)]
@@ -158,45 +185,68 @@ def tile_layernormgrucell_pb_kernel(tc, x, h, r, z, W_in, b_in, W_hn, b_hn, out)
               keep.tile([P, 2 * N], U8, name="sh", align_bytes=64))
 
         win_q = prepare_weight(win_raw, "win", (0, 2, 4, 6))
+        spread_biases()
         for t in range(NT):
             prepare_rows(x_raw, t, xq[0], xq[1])
             product_plus_bias(0, t, xq, win_q, a_t[t])
-            deviation_squares(0, t, a_t[t])
         whn_q = prepare_weight(whn_raw, "whn", ())
         for t in range(NT):
             prepare_rows(h_raw, t, hq[0], hq[1])
+        for t in range(NB):
+            deviation_squares(0, t, a_t[t])
         for t in range(NT):
             product_plus_bias(1, t, hq, whn_q, c_t[t])
-            deviation_squares(1, t, c_t[t])
+            mean_of(1, t)
+            if t < NB:
+                squares_of(1, t, c_t[t])
 
-        def tile_of(raw, t):
-            return raw[t // 2][:, (t % 2) * N:(t % 2 + 1) * N]
-
-        for t in range(NT):
+        def reset_gate(t):
             nc.vector.scalar_tensor_tensor(out=c_t[t][:], in0=c_t[t][:], scalar=nmu[:, NT + t:NT + t + 1],
                                            in1=tile_of(r_raw, t), op0=ALU.add, op1=ALU.mult)
 
-        nc.scalar.activation(out=std[:], in_=ssq[:], func=ACT.Sqrt, bias=eps_t[:], scale=1.0 / N)
-        nc.scalar.activation(out=scr[:, 0:1], in_=eps_t[:], func=ACT.Tanh)
-        nc.vector.reciprocal(out=rho[:], in_=std[:])
-        nc.vector.tensor_tensor(out=kap[:], in0=rho[:, NT:2 * NT], in1=std[:, 0:NT], op=ALU.mult)
-        nc.vector.tensor_tensor(out=nb[:], in0=nmu[:, 0:NT], in1=rho[:, 0:NT], op=ALU.mult)
+        for t in range(NB):
+            reset_gate(t)
+
+        def row_scales(lo, hi):
+            def both(ap):
+                return ap.rearrange("p (m t) -> p m t", m=2)[:, :, lo:hi]
+            nc.scalar.activation(out=both(std[:]), in_=both(ssq[:]), func=ACT.Sqrt, bias=eps_t[:], scale=1.0 / N)
+            nc.scalar.activation(out=scr[:, 0:1], in_=eps_t[:], func=ACT.Tanh)
+            nc.vector.reciprocal(out=both(rho[:]), in_=both(std[:]))
+            nc.vector.tensor_tensor(out=kap[:, lo:hi], in0=rho[:, NT + lo:NT + hi], in1=std[:, lo:hi], op=ALU.mult)
+            nc.vector.tensor_tensor(out=nb[:, lo:hi], in0=nmu[:, lo:hi], in1=rho[:, lo:hi], op=ALU.mult)
 
         def candidate(t):
             nc.vector.scalar_tensor_tensor(out=a_t[t][:], in0=c_t[t][:], scalar=kap[:, t:t + 1],
                                            in1=a_t[t][:], op0=ALU.mult, op1=ALU.add)
             nc.scalar.activation(out=a_t[t][:], in_=a_t[t][:], func=ACT.Tanh,
                                  bias=nb[:, t:t + 1], scale=rho[:, t:t + 1])
-            nc.vector.tensor_tensor(out=c_t[t][:], in0=tile_of(z_raw, t), in1=tile_of(h_raw, t), op=ALU.mult)
 
-        def blend(t):
-            nc.vector.scalar_tensor_tensor(out=a_t[t][:], in0=tile_of(z_raw, t), scalar=1.0,
-                                           in1=a_t[t][:], op0=ALU.subtract, op1=ALU.mult)
-            nc.vector.tensor_tensor(out=a_t[t][:], in0=c_t[t][:], in1=a_t[t][:], op=ALU.subtract)
-            nc.sync.dma_start(out=out_v[:, t, :], in_=a_t[t][:])
+        def blend(t, pieces):
+            w = N // pieces
+            for i in range(pieces):
+                cols = slice(i * w, (i + 1) * w)
+                nc.vector.scalar_tensor_tensor(out=a_t[t][:, cols], in0=tile_of(z_raw, t)[:, cols], scalar=1.0,
+                                               in1=a_t[t][:, cols], op0=ALU.subtract, op1=ALU.mult)
+                nc.vector.tensor_tensor(out=a_t[t][:, cols], in0=zh_t[t][:, cols], in1=a_t[t][:, cols],
+                                        op=ALU.subtract)
+                nc.sync.dma_start(out=out_v[:, t, cols], in_=a_t[t][:, cols])
 
+        row_scales(0, NB)
         candidate(0)
-        for t in range(1, NT):
+        for t in range(1, NB):
             candidate(t)
-            blend(t - 1)
-        blend(NT - 1)
+            blend(t - 1, 1)
+        for t in range(NB, NT):
+            squares_of(1, t, c_t[t])
+        for t in range(NB, NT):
+            deviation_squares(0, t, a_t[t])
+        blend(NB - 1, 1)
+        for t in range(NB, NT):
+            reset_gate(t)
+        row_scales(NB, NT)
+        candidate(NB)
+        for t in range(NB + 1, NT):
+            candidate(t)
+            blend(t - 1, 1)
+        blend(NT - 1, 2)

@@ -19,6 +19,7 @@ HALF = 512
 EPS = 1e-5
 FLOPS = 2 * 2 * N * N * N
 PIN = False
+G_LAST = (0, 2, 4, 6)
 NB = 4
 
 
@@ -40,6 +41,8 @@ def tile_layernormgrucell_pb_kernel(tc, x, h, r, z, W_in, b_in, W_hn, b_hn, out)
         make_identity(nc, ident[:])
         ones = const.tile([P, P], BF16, name="ones")
         nc.vector.memset(ones[:], 1.0)
+        ident_bf = const.tile([P, P], BF16, name="ident_bf")
+        make_identity(nc, ident_bf[:])
         eps_t = const.tile([P, 1], F32, name="eps_t")
         nc.vector.memset(eps_t[:], EPS)
         scr = const.tile([P, 2], F32, name="scr")
@@ -223,14 +226,21 @@ def tile_layernormgrucell_pb_kernel(tc, x, h, r, z, W_in, b_in, W_hn, b_hn, out)
                                  bias=nb[:, t:t + 1], scale=rho[:, t:t + 1])
 
         def blend(t, pieces):
-            w = N // pieces
-            for i in range(pieces):
-                cols = slice(i * w, (i + 1) * w)
-                nc.vector.scalar_tensor_tensor(out=a_t[t][:, cols], in0=tile_of(z_raw, t)[:, cols], scalar=1.0,
+            for i in range(2):
+                cols = slice(i * HALF, (i + 1) * HALF)
+                zp = mxp.tile([P, HALF], F32, name="zp", tag="mx")
+                nc.tensor.matmul(out=zp[:], lhsT=ident_bf[:], rhs=tile_of(z_raw, t)[:, cols], start=True, stop=True)
+                nc.vector.scalar_tensor_tensor(out=a_t[t][:, cols], in0=zp[:], scalar=1.0,
                                                in1=a_t[t][:, cols], op0=ALU.subtract, op1=ALU.mult)
-                nc.vector.tensor_tensor(out=a_t[t][:, cols], in0=zh_t[t][:, cols], in1=a_t[t][:, cols],
-                                        op=ALU.subtract)
-                nc.sync.dma_start(out=out_v[:, t, cols], in_=a_t[t][:, cols])
+            eng = nc.gpsimd if t in G_LAST else nc.vector
+            cuts = 2 if t in G_LAST else pieces
+            for i in range(cuts):
+                cols = slice(i * (N // cuts), (i + 1) * (N // cuts))
+                eng.tensor_tensor(out=a_t[t][:, cols], in0=zh_t[t][:, cols], in1=a_t[t][:, cols], op=ALU.subtract)
+                if pieces == 2:
+                    nc.sync.dma_start(out=out_v[:, t, cols], in_=a_t[t][:, cols])
+            if pieces == 1:
+                nc.sync.dma_start(out=out_v[:, t, :], in_=a_t[t][:])
 
         row_scales(0, NB)
         candidate(0)

@@ -19,8 +19,8 @@ HALF = 512
 EPS = 1e-5
 FLOPS = 2 * 2 * N * N * N
 PIN = False
-G_LAST = (0, 2, 4, 6)
-NB = 4
+BATCHES = ((0, 1, 2, 3), (4, 5, 6, 7))
+G_LAST = (0, 1, 4)
 
 
 def tile_layernormgrucell_pb_kernel(tc, x, h, r, z, W_in, b_in, W_hn, b_hn, out):
@@ -136,17 +136,17 @@ def tile_layernormgrucell_pb_kernel(tc, x, h, r, z, W_in, b_in, W_hn, b_hn, out)
                     c = 4 * half + c4
                     tp = transpose_block(raw[c // 2], c % 2)
                     evacuate(c in vector_chunks, tp, gview[:, :, c4, :, :])
-                for g in range(2):
-                    cols = slice(g * N + half * HALF, g * N + (half + 1) * HALF)
-                    nc.vector.quantize_mx(out=codes[:, cols].bitcast(FP8X4), scales=scales[:, cols],
-                                          in_=gw[:, g * 2 * N:(g + 1) * 2 * N])
+                cols = slice(half * N, (half + 1) * N)
+                nc.vector.quantize_mx(out=codes[:, cols].bitcast(FP8X4), scales=scales[:, cols], in_=gw[:])
             return codes, scales
 
-        def prepare_rows(raw, t, codes, scales):
-            tp = transpose_block(raw[t // 2], t % 2)
-            gx = grp.tile([P, N], BF16, name="gx", tag="gx", bufs=2, align_bytes=64)
-            evacuate(False, tp, gx[:].bitcast(F32).rearrange("p (g r u) -> p g r u", g=2, u=2))
-            cols = slice(t * 2 * P, (t + 1) * 2 * P)
+        def prepare_rows(raw, pair, codes, scales):
+            gx = grp.tile([P, 2 * N], BF16, name="gx", tag="gx", align_bytes=64)
+            gview = gx[:].bitcast(F32).rearrange("p (t g r u) -> p t g r u", t=2, g=2, u=2)
+            for cc in range(2):
+                tp = transpose_block(raw[pair], cc)
+                evacuate(False, tp, gview[:, cc, :, :, :])
+            cols = slice(pair * 4 * P, (pair + 1) * 4 * P)
             nc.vector.quantize_mx(out=codes[:, cols].bitcast(FP8X4), scales=scales[:, cols], in_=gx[:])
 
         def product_plus_bias(m, t, rows, weight, dst):
@@ -156,7 +156,7 @@ def tile_layernormgrucell_pb_kernel(tc, x, h, r, z, W_in, b_in, W_hn, b_hn, out)
                 ps = mxp.tile([P, HALF], F32, name="ps", tag="mx")
                 for g in range(2):
                     lcols = slice(t * 2 * P + g * P, t * 2 * P + (g + 1) * P)
-                    rcols = slice(g * N + half * HALF, g * N + (half + 1) * HALF)
+                    rcols = slice(half * N + g * HALF, half * N + (g + 1) * HALF)
                     nc.tensor.matmul_mx(out=ps[:], lhsT=rc[:, lcols].bitcast(FP8X4), lhsT_scale=rs[:, lcols],
                                         rhs=wc[:, rcols].bitcast(FP8X4), rhs_scale=ws[:, rcols],
                                         start=(g == 0), stop=(g == 1))
@@ -176,10 +176,6 @@ def tile_layernormgrucell_pb_kernel(tc, x, h, r, z, W_in, b_in, W_hn, b_hn, out)
             nc.scalar.activation(out=junk[:], in_=src[:], func=ACT.Square, bias=nmu[:, i:i + 1],
                                  scale=1.0, accum_out=ssq[:, i:i + 1])
 
-        def deviation_squares(m, t, src):
-            mean_of(m, t)
-            squares_of(m, t, src)
-
         a_t = [keep.tile([P, N], F32, name="a%d" % t) for t in range(NT)]
         c_t = [keep.tile([P, N], F32, name="c%d" % t) for t in range(NT)]
         xq = (keep.tile([P, 2 * N], U32, name="cx", align_bytes=64),
@@ -189,26 +185,21 @@ def tile_layernormgrucell_pb_kernel(tc, x, h, r, z, W_in, b_in, W_hn, b_hn, out)
 
         win_q = prepare_weight(win_raw, "win", (0, 2, 4, 6))
         spread_biases()
-        for t in range(NT):
-            prepare_rows(x_raw, t, xq[0], xq[1])
-            product_plus_bias(0, t, xq, win_q, a_t[t])
+        for pair in range(NT // 2):
+            prepare_rows(x_raw, pair, xq[0], xq[1])
+            for t in (2 * pair, 2 * pair + 1):
+                product_plus_bias(0, t, xq, win_q, a_t[t])
         whn_q = prepare_weight(whn_raw, "whn", ())
-        for t in range(NT):
-            prepare_rows(h_raw, t, hq[0], hq[1])
-        for t in range(NB):
-            deviation_squares(0, t, a_t[t])
+        for pair in range(NT // 2):
+            prepare_rows(h_raw, pair, hq[0], hq[1])
+        for t in BATCHES[0]:
+            mean_of(0, t)
+            squares_of(0, t, a_t[t])
         for t in range(NT):
             product_plus_bias(1, t, hq, whn_q, c_t[t])
             mean_of(1, t)
-            if t < NB:
+            if t in BATCHES[0]:
                 squares_of(1, t, c_t[t])
-
-        def reset_gate(t):
-            nc.vector.scalar_tensor_tensor(out=c_t[t][:], in0=c_t[t][:], scalar=nmu[:, NT + t:NT + t + 1],
-                                           in1=tile_of(r_raw, t), op0=ALU.add, op1=ALU.mult)
-
-        for t in range(NB):
-            reset_gate(t)
 
         def row_scales(lo, hi):
             def both(ap):
@@ -219,44 +210,43 @@ def tile_layernormgrucell_pb_kernel(tc, x, h, r, z, W_in, b_in, W_hn, b_hn, out)
             nc.vector.tensor_tensor(out=kap[:, lo:hi], in0=rho[:, NT + lo:NT + hi], in1=std[:, lo:hi], op=ALU.mult)
             nc.vector.tensor_tensor(out=nb[:, lo:hi], in0=nmu[:, lo:hi], in1=rho[:, lo:hi], op=ALU.mult)
 
-        def candidate(t):
-            nc.vector.scalar_tensor_tensor(out=a_t[t][:], in0=c_t[t][:], scalar=kap[:, t:t + 1],
-                                           in1=a_t[t][:], op0=ALU.mult, op1=ALU.add)
-            nc.scalar.activation(out=a_t[t][:], in_=a_t[t][:], func=ACT.Tanh,
-                                 bias=nb[:, t:t + 1], scale=rho[:, t:t + 1])
-
-        def blend(t, pieces):
-            for i in range(2):
-                cols = slice(i * HALF, (i + 1) * HALF)
-                zp = mxp.tile([P, HALF], F32, name="zp", tag="mx")
-                nc.tensor.matmul(out=zp[:], lhsT=ident_bf[:], rhs=tile_of(z_raw, t)[:, cols], start=True, stop=True)
-                nc.vector.scalar_tensor_tensor(out=a_t[t][:, cols], in0=zp[:], scalar=1.0,
-                                               in1=a_t[t][:, cols], op0=ALU.subtract, op1=ALU.mult)
-            eng = nc.gpsimd if t in G_LAST else nc.vector
-            cuts = 2 if t in G_LAST else pieces
-            for i in range(cuts):
-                cols = slice(i * (N // cuts), (i + 1) * (N // cuts))
-                eng.tensor_tensor(out=a_t[t][:, cols], in0=zh_t[t][:, cols], in1=a_t[t][:, cols], op=ALU.subtract)
-                if pieces == 2:
-                    nc.sync.dma_start(out=out_v[:, t, cols], in_=a_t[t][:, cols])
-            if pieces == 1:
-                nc.sync.dma_start(out=out_v[:, t, :], in_=a_t[t][:])
-
-        row_scales(0, NB)
-        candidate(0)
-        for t in range(1, NB):
-            candidate(t)
-            blend(t - 1, 1)
-        for t in range(NB, NT):
-            squares_of(1, t, c_t[t])
-        for t in range(NB, NT):
-            deviation_squares(0, t, a_t[t])
-        blend(NB - 1, 1)
-        for t in range(NB, NT):
-            reset_gate(t)
-        row_scales(NB, NT)
-        candidate(NB)
-        for t in range(NB + 1, NT):
-            candidate(t)
-            blend(t - 1, 1)
-        blend(NT - 1, 2)
+        for b in range(len(BATCHES)):
+            tiles = BATCHES[b]
+            for t in tiles:
+                nc.vector.scalar_tensor_tensor(out=c_t[t][:], in0=c_t[t][:], scalar=nmu[:, NT + t:NT + t + 1],
+                                               in1=tile_of(r_raw, t), op0=ALU.add, op1=ALU.mult)
+            row_scales(tiles[0], tiles[-1] + 1)
+            for t in tiles:
+                nc.vector.scalar_tensor_tensor(out=a_t[t][:], in0=c_t[t][:], scalar=kap[:, t:t + 1],
+                                               in1=a_t[t][:], op0=ALU.mult, op1=ALU.add)
+                nc.scalar.activation(out=a_t[t][:], in_=a_t[t][:], func=ACT.Tanh,
+                                     bias=nb[:, t:t + 1], scale=rho[:, t:t + 1])
+            if b + 1 < len(BATCHES):
+                for t in BATCHES[b + 1]:
+                    squares_of(1, t, c_t[t])
+                for t in BATCHES[b + 1]:
+                    mean_of(0, t)
+                    squares_of(0, t, a_t[t])
+            for t in tiles:
+                for i in range(2):
+                    cols = slice(i * HALF, (i + 1) * HALF)
+                    if t % 2 == 0:
+                        zp = mxp.tile([P, HALF], F32, name="zp", tag="mx")
+                    else:
+                        zp = tpp.tile([P, HALF], F32, name="zq", tag="tp")
+                    nc.tensor.matmul(out=zp[:], lhsT=ident_bf[:], rhs=tile_of(z_raw, t)[:, cols],
+                                     start=True, stop=True)
+                    nc.vector.scalar_tensor_tensor(out=a_t[t][:, cols], in0=zp[:], scalar=1.0,
+                                                   in1=a_t[t][:, cols], op0=ALU.subtract, op1=ALU.mult)
+            for t in tiles:
+                last = t == NT - 1
+                eng = nc.gpsimd if t in G_LAST else nc.vector
+                cuts = 2 if (t in G_LAST or last) else 1
+                for i in range(cuts):
+                    cols = slice(i * (N // cuts), (i + 1) * (N // cuts))
+                    eng.tensor_tensor(out=a_t[t][:, cols], in0=zh_t[t][:, cols], in1=a_t[t][:, cols],
+                                      op=ALU.subtract)
+                    if last:
+                        nc.sync.dma_start(out=out_v[:, t, cols], in_=a_t[t][:, cols])
+                if not last:
+                    nc.sync.dma_start(out=out_v[:, t, :], in_=a_t[t][:])

@@ -18,16 +18,15 @@ NT = N // P
 HALF = 512
 EPS = 1e-5
 FLOPS = 2 * 2 * N * N * N
-PIN = False
 BATCHES = ((0, 1, 2, 3), (4, 5, 6, 7))
 G_LAST = (0, 1, 4)
+V_CHUNKS = (0, 2, 4, 6)
 
 
 def tile_layernormgrucell_pb_kernel(tc, x, h, r, z, W_in, b_in, W_hn, b_hn, out):
     nc = tc.nc
     with ExitStack() as ctx:
-        if PIN:
-            ctx.enter_context(tc.manual_schedule())
+        ctx.enter_context(tc.manual_schedule())
         const = ctx.enter_context(tc.tile_pool(name="const", bufs=1))
         rawp = ctx.enter_context(tc.tile_pool(name="raw", bufs=4))
         grp = ctx.enter_context(tc.tile_pool(name="grouped", bufs=2))
@@ -47,8 +46,6 @@ def tile_layernormgrucell_pb_kernel(tc, x, h, r, z, W_in, b_in, W_hn, b_hn, out)
         nc.vector.memset(eps_t[:], EPS)
         scr = const.tile([P, 2], F32, name="scr")
         nc.scalar.activation(out=scr[:, 0:1], in_=eps_t[:], func=ACT.Sqrt)
-        nc.sync.dma_start(out=zb[0:1, 0:N], in_=b_in.rearrange("(o n) -> o n", o=1))
-        nc.sync.dma_start(out=zb[0:1, N:2 * N], in_=b_hn.rearrange("(o n) -> o n", o=1))
 
         bias = const.tile([P, 2 * N], F32, name="bias")
         sums = const.tile([P, 4 * NT], F32, name="sums")
@@ -60,11 +57,6 @@ def tile_layernormgrucell_pb_kernel(tc, x, h, r, z, W_in, b_in, W_hn, b_hn, out)
         nb = const.tile([P, NT], F32, name="nb")
         junk = const.tile([P, N], BF16, name="junk")
 
-        w_views = [W_in.rearrange("(c p) k -> p c k", p=P), W_hn.rearrange("(c p) k -> p c k", p=P)]
-        x_v = x.rearrange("(p t) k -> p t k", t=NT)
-        h_v = h.rearrange("(p t) k -> p t k", t=NT)
-        r_v = r.rearrange("(p t) k -> p t k", t=NT)
-        z_v = z.rearrange("(p t) k -> p t k", t=NT)
         out_v = out.rearrange("(p t) k -> p t k", t=NT)
 
         def load_pairs(view, tag, resident):
@@ -77,14 +69,19 @@ def tile_layernormgrucell_pb_kernel(tc, x, h, r, z, W_in, b_in, W_hn, b_hn, out)
                 nc.sync.dma_start(out=t_[:].rearrange("p (c k) -> p c k", c=2),
                                   in_=view[:, 2 * i:2 * i + 2, :])
                 tiles.append(t_)
+                if tag == "wwin" and i == 1:
+                    nc.sync.dma_start(out=zb[0:1, 0:N], in_=b_in.rearrange("(o n) -> o n", o=1))
+                    nc.sync.dma_start(out=zb[0:1, N:2 * N], in_=b_hn.rearrange("(o n) -> o n", o=1))
             return tiles
 
-        win_raw = load_pairs(w_views[0], "wwin", False)
-        x_raw = load_pairs(x_v, "xrx", False)
-        whn_raw = load_pairs(w_views[1], "wwhn", False)
-        h_raw = load_pairs(h_v, "hraw", True)
-        z_raw = load_pairs(z_v, "zraw", True)
-        r_raw = load_pairs(r_v, "xrr", False)
+        win_raw = load_pairs(W_in.rearrange("(c p) k -> p c k", p=P), "wwin", False)
+        x_raw = load_pairs(x.rearrange("(p t) k -> p t k", t=NT), "xrx", False)
+        whn_raw = load_pairs(W_hn.rearrange("(c p) k -> p c k", p=P), "wwhn", False)
+        h_raw = load_pairs(h.rearrange("(p t) k -> p t k", t=NT), "hraw", True)
+        z_raw = load_pairs(z.rearrange("(p t) k -> p t k", t=NT), "zraw", True)
+        r_raw = load_pairs(r.rearrange("(p t) k -> p t k", t=NT), "xrr", False)
+        w_raw = (win_raw, whn_raw)
+        row_raw = (x_raw, h_raw)
 
         def tile_of(raw, t):
             return raw[t // 2][:, (t % 2) * N:(t % 2 + 1) * N]
@@ -101,68 +98,80 @@ def tile_layernormgrucell_pb_kernel(tc, x, h, r, z, W_in, b_in, W_hn, b_hn, out)
                                         in1=tile_of(h_raw, t)[:, cols], op=ALU.mult)
             zh_t.append(zh)
 
+        acc = ([keep.tile([P, N], F32, name="a%d" % t) for t in range(NT)],
+               [keep.tile([P, N], F32, name="c%d" % t) for t in range(NT)])
+        a_t, c_t = acc
+        w_codes = [keep.tile([P, 2 * N], U32, name="cw%d" % m, align_bytes=64) for m in range(2)]
+        w_scales = [keep.tile([P, 2 * N], U8, name="sw%d" % m, align_bytes=64) for m in range(2)]
+        r_codes = [keep.tile([P, 2 * N], U32, name="cr%d" % m, align_bytes=64) for m in range(2)]
+        r_scales = [keep.tile([P, 2 * N], U8, name="sr%d" % m, align_bytes=64) for m in range(2)]
+        grouped = {}
+        banks = {}
+
         def spread_biases():
             for k in range(4):
                 ps = mxp.tile([P, HALF], F32, name="ps", tag="mx")
                 nc.tensor.matmul(out=ps[:], lhsT=ones[:], rhs=zb[:, k * HALF:(k + 1) * HALF],
                                  start=True, stop=True)
-                if k % 2 == 0:
+                if k < 2:
                     nc.vector.tensor_copy(out=bias[:, k * HALF:(k + 1) * HALF], in_=ps[:])
                 else:
                     nc.scalar.copy(out=bias[:, k * HALF:(k + 1) * HALF], in_=ps[:])
 
-        def transpose_block(raw_pair, cc):
+        def transpose_out(raw_pair, cc, on_vector, dst):
             tp = tpp.tile([P, HALF], F32, name="tp", tag="tp")
             words = raw_pair[:].bitcast(F32)
             for q in range(4):
                 nc.tensor.transpose(tp[:, q * P:(q + 1) * P],
                                     words[:, cc * HALF + q * P:cc * HALF + (q + 1) * P], ident[:])
-            return tp
-
-        def evacuate(on_vector, tp, dst):
             src = tp[:].rearrange("p (g u r) -> p g r u", g=2, u=2)
             if on_vector:
                 nc.vector.tensor_copy(out=dst, in_=src)
             else:
                 nc.scalar.copy(out=dst, in_=src)
 
-        def prepare_weight(raw, name, vector_chunks):
-            codes = keep.tile([P, 2 * N], U32, name="c" + name, align_bytes=64)
-            scales = keep.tile([P, 2 * N], U8, name="s" + name, align_bytes=64)
-            for half in range(2):
-                gw = grp.tile([P, 4 * N], BF16, name="gw", tag="gw", align_bytes=64)
-                gview = gw[:].bitcast(F32).rearrange("p (g c r u) -> p g c r u", g=2, c=4, u=2)
-                for c4 in range(4):
-                    c = 4 * half + c4
-                    tp = transpose_block(raw[c // 2], c % 2)
-                    evacuate(c in vector_chunks, tp, gview[:, :, c4, :, :])
-                cols = slice(half * N, (half + 1) * N)
-                nc.vector.quantize_mx(out=codes[:, cols].bitcast(FP8X4), scales=scales[:, cols], in_=gw[:])
-            return codes, scales
+        def t_weight(m, half):
+            gw = grp.tile([P, 4 * N], BF16, name="gw", tag="gw", align_bytes=64)
+            grouped[("w", m, half)] = gw
+            gview = gw[:].bitcast(F32).rearrange("p (g c r u) -> p g c r u", g=2, c=4, u=2)
+            for c4 in range(4):
+                c = 4 * half + c4
+                transpose_out(w_raw[m][c // 2], c % 2, m == 0 and c in V_CHUNKS, gview[:, :, c4, :, :])
 
-        def prepare_rows(raw, pair, codes, scales):
-            gx = grp.tile([P, 2 * N], BF16, name="gx", tag="gx", align_bytes=64)
+        def q_weight(m, half):
+            cols = slice(half * N, (half + 1) * N)
+            nc.vector.quantize_mx(out=w_codes[m][:, cols].bitcast(FP8X4), scales=w_scales[m][:, cols],
+                                  in_=grouped[("w", m, half)][:])
+
+        def t_rows(m, pair):
+            gx = grp.tile([P, 2 * N], BF16, name="gx", tag="gx", bufs=3, align_bytes=64)
+            grouped[("r", m, pair)] = gx
             gview = gx[:].bitcast(F32).rearrange("p (t g r u) -> p t g r u", t=2, g=2, u=2)
             for cc in range(2):
-                tp = transpose_block(raw[pair], cc)
-                evacuate(False, tp, gview[:, cc, :, :, :])
-            cols = slice(pair * 4 * P, (pair + 1) * 4 * P)
-            nc.vector.quantize_mx(out=codes[:, cols].bitcast(FP8X4), scales=scales[:, cols], in_=gx[:])
+                transpose_out(row_raw[m][pair], cc, False, gview[:, cc, :, :, :])
 
-        def product_plus_bias(m, t, rows, weight, dst):
-            rc, rs = rows
-            wc, ws = weight
+        def q_rows(m, pair):
+            cols = slice(pair * 4 * P, (pair + 1) * 4 * P)
+            nc.vector.quantize_mx(out=r_codes[m][:, cols].bitcast(FP8X4), scales=r_scales[m][:, cols],
+                                  in_=grouped[("r", m, pair)][:])
+
+        def product(m, t):
             for half in range(2):
                 ps = mxp.tile([P, HALF], F32, name="ps", tag="mx")
+                banks[(m, t, half)] = ps
                 for g in range(2):
                     lcols = slice(t * 2 * P + g * P, t * 2 * P + (g + 1) * P)
                     rcols = slice(half * N + g * HALF, half * N + (g + 1) * HALF)
-                    nc.tensor.matmul_mx(out=ps[:], lhsT=rc[:, lcols].bitcast(FP8X4), lhsT_scale=rs[:, lcols],
-                                        rhs=wc[:, rcols].bitcast(FP8X4), rhs_scale=ws[:, rcols],
+                    nc.tensor.matmul_mx(out=ps[:], lhsT=r_codes[m][:, lcols].bitcast(FP8X4),
+                                        lhsT_scale=r_scales[m][:, lcols],
+                                        rhs=w_codes[m][:, rcols].bitcast(FP8X4), rhs_scale=w_scales[m][:, rcols],
                                         start=(g == 0), stop=(g == 1))
+
+        def add_bias(m, t):
+            for half in range(2):
                 k = (m * NT + t) * 2 + half
                 nc.vector.scalar_tensor_tensor(
-                    out=dst[:, half * HALF:(half + 1) * HALF], in0=ps[:], scalar=1.0,
+                    out=acc[m][t][:, half * HALF:(half + 1) * HALF], in0=banks[(m, t, half)][:], scalar=1.0,
                     in1=bias[:, m * N + half * HALF:m * N + (half + 1) * HALF],
                     op0=ALU.mult, op1=ALU.add, accum_out=sums[:, k:k + 1])
 
@@ -171,35 +180,10 @@ def tile_layernormgrucell_pb_kernel(tc, x, h, r, z, W_in, b_in, W_hn, b_hn, out)
             nc.scalar.activation(out=scr[:, 0:2], in_=sums[:, 2 * i:2 * i + 2], func=ACT.Identity,
                                  scale=-1.0 / N, accum_out=nmu[:, i:i + 1])
 
-        def squares_of(m, t, src):
+        def squares_of(m, t):
             i = m * NT + t
-            nc.scalar.activation(out=junk[:], in_=src[:], func=ACT.Square, bias=nmu[:, i:i + 1],
+            nc.scalar.activation(out=junk[:], in_=acc[m][t][:], func=ACT.Square, bias=nmu[:, i:i + 1],
                                  scale=1.0, accum_out=ssq[:, i:i + 1])
-
-        a_t = [keep.tile([P, N], F32, name="a%d" % t) for t in range(NT)]
-        c_t = [keep.tile([P, N], F32, name="c%d" % t) for t in range(NT)]
-        xq = (keep.tile([P, 2 * N], U32, name="cx", align_bytes=64),
-              keep.tile([P, 2 * N], U8, name="sx", align_bytes=64))
-        hq = (keep.tile([P, 2 * N], U32, name="ch", align_bytes=64),
-              keep.tile([P, 2 * N], U8, name="sh", align_bytes=64))
-
-        win_q = prepare_weight(win_raw, "win", (0, 2, 4, 6))
-        spread_biases()
-        for pair in range(NT // 2):
-            prepare_rows(x_raw, pair, xq[0], xq[1])
-            for t in (2 * pair, 2 * pair + 1):
-                product_plus_bias(0, t, xq, win_q, a_t[t])
-        whn_q = prepare_weight(whn_raw, "whn", ())
-        for pair in range(NT // 2):
-            prepare_rows(h_raw, pair, hq[0], hq[1])
-        for t in BATCHES[0]:
-            mean_of(0, t)
-            squares_of(0, t, a_t[t])
-        for t in range(NT):
-            product_plus_bias(1, t, hq, whn_q, c_t[t])
-            mean_of(1, t)
-            if t in BATCHES[0]:
-                squares_of(1, t, c_t[t])
 
         def row_scales(lo, hi):
             def both(ap):
@@ -210,12 +194,72 @@ def tile_layernormgrucell_pb_kernel(tc, x, h, r, z, W_in, b_in, W_hn, b_hn, out)
             nc.vector.tensor_tensor(out=kap[:, lo:hi], in0=rho[:, NT + lo:NT + hi], in1=std[:, lo:hi], op=ALU.mult)
             nc.vector.tensor_tensor(out=nb[:, lo:hi], in0=nmu[:, lo:hi], in1=rho[:, lo:hi], op=ALU.mult)
 
+        t_weight(0, 0)
+        spread_biases()
+        q_weight(0, 0)
+        t_weight(0, 1)
+        t_rows(0, 0)
+        t_rows(0, 1)
+        q_weight(0, 1)
+        t_rows(0, 2)
+        t_rows(0, 3)
+        q_rows(0, 0)
+        q_rows(0, 1)
+
+        product(0, 0)
+        product(0, 1)
+        t_weight(1, 0)
+        add_bias(0, 0)
+        add_bias(0, 1)
+        q_rows(0, 2)
+        q_rows(0, 3)
+
+        product(0, 2)
+        product(0, 3)
+        t_weight(1, 1)
+        add_bias(0, 2)
+        add_bias(0, 3)
+        q_weight(1, 0)
+
+        product(0, 4)
+        product(0, 5)
+        t_rows(1, 0)
+        t_rows(1, 1)
+        add_bias(0, 4)
+        add_bias(0, 5)
+        q_weight(1, 1)
+
+        product(0, 6)
+        product(0, 7)
+        t_rows(1, 2)
+        t_rows(1, 3)
+        add_bias(0, 6)
+        add_bias(0, 7)
+        for pair in range(NT // 2):
+            q_rows(1, pair)
+
+        product(1, 0)
+        product(1, 1)
+        for t in BATCHES[0]:
+            mean_of(0, t)
+            squares_of(0, t)
+        for t in range(NT):
+            add_bias(1, t)
+            if t + 2 < NT:
+                product(1, t + 2)
+            mean_of(1, t)
+            if t in BATCHES[0]:
+                squares_of(1, t)
+
         for b in range(len(BATCHES)):
             tiles = BATCHES[b]
             for t in tiles:
                 nc.vector.scalar_tensor_tensor(out=c_t[t][:], in0=c_t[t][:], scalar=nmu[:, NT + t:NT + t + 1],
                                                in1=tile_of(r_raw, t), op0=ALU.add, op1=ALU.mult)
             row_scales(tiles[0], tiles[-1] + 1)
+            if b + 1 < len(BATCHES):
+                for t in BATCHES[b + 1]:
+                    squares_of(1, t)
             for t in tiles:
                 nc.vector.scalar_tensor_tensor(out=a_t[t][:], in0=c_t[t][:], scalar=kap[:, t:t + 1],
                                                in1=a_t[t][:], op0=ALU.mult, op1=ALU.add)
@@ -223,10 +267,8 @@ def tile_layernormgrucell_pb_kernel(tc, x, h, r, z, W_in, b_in, W_hn, b_hn, out)
                                      bias=nb[:, t:t + 1], scale=rho[:, t:t + 1])
             if b + 1 < len(BATCHES):
                 for t in BATCHES[b + 1]:
-                    squares_of(1, t, c_t[t])
-                for t in BATCHES[b + 1]:
                     mean_of(0, t)
-                    squares_of(0, t, a_t[t])
+                    squares_of(0, t)
             for t in tiles:
                 for i in range(2):
                     cols = slice(i * HALF, (i + 1) * HALF)
@@ -234,19 +276,33 @@ def tile_layernormgrucell_pb_kernel(tc, x, h, r, z, W_in, b_in, W_hn, b_hn, out)
                         zp = mxp.tile([P, HALF], F32, name="zp", tag="mx")
                     else:
                         zp = tpp.tile([P, HALF], F32, name="zq", tag="tp")
+                    banks[("z", t, i)] = zp
                     nc.tensor.matmul(out=zp[:], lhsT=ident_bf[:], rhs=tile_of(z_raw, t)[:, cols],
                                      start=True, stop=True)
-                    nc.vector.scalar_tensor_tensor(out=a_t[t][:, cols], in0=zp[:], scalar=1.0,
+            for t in tiles:
+                for i in range(2):
+                    cols = slice(i * HALF, (i + 1) * HALF)
+                    nc.vector.scalar_tensor_tensor(out=a_t[t][:, cols], in0=banks[("z", t, i)][:], scalar=1.0,
                                                    in1=a_t[t][:, cols], op0=ALU.subtract, op1=ALU.mult)
             for t in tiles:
-                last = t == NT - 1
-                eng = nc.gpsimd if t in G_LAST else nc.vector
-                cuts = 2 if (t in G_LAST or last) else 1
-                for i in range(cuts):
-                    cols = slice(i * (N // cuts), (i + 1) * (N // cuts))
-                    eng.tensor_tensor(out=a_t[t][:, cols], in0=zh_t[t][:, cols], in1=a_t[t][:, cols],
-                                      op=ALU.subtract)
-                    if last:
+                if t in G_LAST:
+                    for i in range(2):
+                        cols = slice(i * HALF, (i + 1) * HALF)
+                        nc.gpsimd.tensor_tensor(out=a_t[t][:, cols], in0=zh_t[t][:, cols], in1=a_t[t][:, cols],
+                                                op=ALU.subtract)
+            if b + 1 == len(BATCHES):
+                for t in tiles:
+                    if t in G_LAST:
+                        nc.sync.dma_start(out=out_v[:, t, :], in_=a_t[t][:])
+            for t in tiles:
+                if t not in G_LAST:
+                    cuts = 2 if t == NT - 1 else 1
+                    for i in range(cuts):
+                        cols = slice(i * (N // cuts), (i + 1) * (N // cuts))
+                        nc.vector.tensor_tensor(out=a_t[t][:, cols], in0=zh_t[t][:, cols], in1=a_t[t][:, cols],
+                                                op=ALU.subtract)
                         nc.sync.dma_start(out=out_v[:, t, cols], in_=a_t[t][:, cols])
-                if not last:
-                    nc.sync.dma_start(out=out_v[:, t, :], in_=a_t[t][:])
+            if b + 1 < len(BATCHES):
+                for t in tiles:
+                    if t in G_LAST:
+                        nc.sync.dma_start(out=out_v[:, t, :], in_=a_t[t][:])

@@ -20,6 +20,7 @@ EPS = 1e-5
 FLOPS = 2 * 2 * N * N * N
 BATCHES = ((0, 1, 2, 3), (4, 5, 6, 7))
 G_LAST = (0, 1, 4)
+W0, W1, W2, W3 = 2, 1, 1, 1
 V_CHUNKS = (0, 2, 4, 6)
 
 
@@ -56,6 +57,7 @@ def tile_layernormgrucell_pb_kernel(tc, x, h, r, z, W_in, b_in, W_hn, b_hn, out)
         kap = const.tile([P, NT], F32, name="kap")
         nb = const.tile([P, NT], F32, name="nb")
         junk = const.tile([P, N], BF16, name="junk")
+        nc.vector.memset(junk[:].bitcast(I32), 0)
 
         out_v = out.rearrange("(p t) k -> p t k", t=NT)
 
@@ -69,16 +71,16 @@ def tile_layernormgrucell_pb_kernel(tc, x, h, r, z, W_in, b_in, W_hn, b_hn, out)
                 nc.sync.dma_start(out=t_[:].rearrange("p (c k) -> p c k", c=2),
                                   in_=view[:, 2 * i:2 * i + 2, :])
                 tiles.append(t_)
-                if tag == "wwin" and i == 1:
+                if tag == "wwin" and i == 0:
                     nc.sync.dma_start(out=zb[0:1, 0:N], in_=b_in.rearrange("(o n) -> o n", o=1))
                     nc.sync.dma_start(out=zb[0:1, N:2 * N], in_=b_hn.rearrange("(o n) -> o n", o=1))
             return tiles
 
         win_raw = load_pairs(W_in.rearrange("(c p) k -> p c k", p=P), "wwin", False)
         x_raw = load_pairs(x.rearrange("(p t) k -> p t k", t=NT), "xrx", False)
-        whn_raw = load_pairs(W_hn.rearrange("(c p) k -> p c k", p=P), "wwhn", False)
         h_raw = load_pairs(h.rearrange("(p t) k -> p t k", t=NT), "hraw", True)
         z_raw = load_pairs(z.rearrange("(p t) k -> p t k", t=NT), "zraw", True)
+        whn_raw = load_pairs(W_hn.rearrange("(c p) k -> p c k", p=P), "wwhn", False)
         r_raw = load_pairs(r.rearrange("(p t) k -> p t k", t=NT), "xrr", False)
         w_raw = (win_raw, whn_raw)
         row_raw = (x_raw, h_raw)
@@ -92,8 +94,8 @@ def tile_layernormgrucell_pb_kernel(tc, x, h, r, z, W_in, b_in, W_hn, b_hn, out)
                 zh = keep.tile([P, N], F32, name="zh%d" % t)
             else:
                 zh = rawp.tile([P, N], F32, name="zh%d" % t, tag="ww")
-            for i in range(2):
-                cols = slice(i * HALF, (i + 1) * HALF)
+            for i in range(4):
+                cols = slice(i * 256, (i + 1) * 256)
                 nc.gpsimd.tensor_tensor(out=zh[:, cols], in0=tile_of(z_raw, t)[:, cols],
                                         in1=tile_of(h_raw, t)[:, cols], op=ALU.mult)
             zh_t.append(zh)
@@ -107,6 +109,11 @@ def tile_layernormgrucell_pb_kernel(tc, x, h, r, z, W_in, b_in, W_hn, b_hn, out)
         r_scales = [keep.tile([P, 2 * N], U8, name="sr%d" % m, align_bytes=64) for m in range(2)]
         grouped = {}
         banks = {}
+
+        def warm(n):
+            ps = mxp.tile([P, HALF], F32, name="ps", tag="mx")
+            for i in range(n):
+                nc.tensor.matmul(out=ps[:], lhsT=ones[:], rhs=junk[:, 0:HALF], start=True, stop=True)
 
         def spread_biases():
             for k in range(4):
@@ -194,49 +201,55 @@ def tile_layernormgrucell_pb_kernel(tc, x, h, r, z, W_in, b_in, W_hn, b_hn, out)
             nc.vector.tensor_tensor(out=kap[:, lo:hi], in0=rho[:, NT + lo:NT + hi], in1=std[:, lo:hi], op=ALU.mult)
             nc.vector.tensor_tensor(out=nb[:, lo:hi], in0=nmu[:, lo:hi], in1=rho[:, lo:hi], op=ALU.mult)
 
-        t_weight(0, 0)
+        warm(W0)
         spread_biases()
+        t_weight(0, 0)
+        warm(W1)
         q_weight(0, 0)
         t_weight(0, 1)
+        warm(W2)
         t_rows(0, 0)
         t_rows(0, 1)
+        warm(W3)
         q_weight(0, 1)
-        t_rows(0, 2)
-        t_rows(0, 3)
         q_rows(0, 0)
         q_rows(0, 1)
 
         product(0, 0)
         product(0, 1)
-        t_weight(1, 0)
+        t_rows(0, 2)
+        t_rows(0, 3)
         add_bias(0, 0)
         add_bias(0, 1)
-        q_rows(0, 2)
-        q_rows(0, 3)
 
         product(0, 2)
         product(0, 3)
-        t_weight(1, 1)
+        t_rows(1, 0)
+        t_rows(1, 1)
         add_bias(0, 2)
         add_bias(0, 3)
-        q_weight(1, 0)
+        q_rows(0, 2)
+        q_rows(0, 3)
 
         product(0, 4)
         product(0, 5)
-        t_rows(1, 0)
-        t_rows(1, 1)
+        t_rows(1, 2)
+        t_rows(1, 3)
         add_bias(0, 4)
         add_bias(0, 5)
-        q_weight(1, 1)
+        q_rows(1, 0)
+        q_rows(1, 1)
 
         product(0, 6)
         product(0, 7)
-        t_rows(1, 2)
-        t_rows(1, 3)
+        t_weight(1, 0)
         add_bias(0, 6)
+        q_rows(1, 2)
+        q_rows(1, 3)
+        t_weight(1, 1)
         add_bias(0, 7)
-        for pair in range(NT // 2):
-            q_rows(1, pair)
+        q_weight(1, 0)
+        q_weight(1, 1)
 
         product(1, 0)
         product(1, 1)

@@ -20,7 +20,6 @@ EPS = 1e-5
 FLOPS = 2 * 2 * N * N * N
 BATCHES = ((0, 1, 2, 3), (4, 5, 6, 7))
 G_LAST = (0, 1, 4)
-W0, W1, W2, W3 = 2, 1, 1, 1
 V_CHUNKS = (0, 2, 4, 6)
 
 
@@ -57,7 +56,6 @@ def tile_layernormgrucell_pb_kernel(tc, x, h, r, z, W_in, b_in, W_hn, b_hn, out)
         kap = const.tile([P, NT], F32, name="kap")
         nb = const.tile([P, NT], F32, name="nb")
         junk = const.tile([P, N], BF16, name="junk")
-        nc.vector.memset(junk[:].bitcast(I32), 0)
 
         out_v = out.rearrange("(p t) k -> p t k", t=NT)
 
@@ -71,7 +69,7 @@ def tile_layernormgrucell_pb_kernel(tc, x, h, r, z, W_in, b_in, W_hn, b_hn, out)
                 nc.sync.dma_start(out=t_[:].rearrange("p (c k) -> p c k", c=2),
                                   in_=view[:, 2 * i:2 * i + 2, :])
                 tiles.append(t_)
-                if tag == "wwin" and i == 0:
+                if tag == "wwin" and i == 1:
                     nc.sync.dma_start(out=zb[0:1, 0:N], in_=b_in.rearrange("(o n) -> o n", o=1))
                     nc.sync.dma_start(out=zb[0:1, N:2 * N], in_=b_hn.rearrange("(o n) -> o n", o=1))
             return tiles
@@ -94,8 +92,8 @@ def tile_layernormgrucell_pb_kernel(tc, x, h, r, z, W_in, b_in, W_hn, b_hn, out)
                 zh = keep.tile([P, N], F32, name="zh%d" % t)
             else:
                 zh = rawp.tile([P, N], F32, name="zh%d" % t, tag="ww")
-            for i in range(4):
-                cols = slice(i * 256, (i + 1) * 256)
+            for i in range(2):
+                cols = slice(i * HALF, (i + 1) * HALF)
                 nc.gpsimd.tensor_tensor(out=zh[:, cols], in0=tile_of(z_raw, t)[:, cols],
                                         in1=tile_of(h_raw, t)[:, cols], op=ALU.mult)
             zh_t.append(zh)
@@ -109,11 +107,6 @@ def tile_layernormgrucell_pb_kernel(tc, x, h, r, z, W_in, b_in, W_hn, b_hn, out)
         r_scales = [keep.tile([P, 2 * N], U8, name="sr%d" % m, align_bytes=64) for m in range(2)]
         grouped = {}
         banks = {}
-
-        def warm(n):
-            ps = mxp.tile([P, HALF], F32, name="ps", tag="mx")
-            for i in range(n):
-                nc.tensor.matmul(out=ps[:], lhsT=ones[:], rhs=junk[:, 0:HALF], start=True, stop=True)
 
         def spread_biases():
             for k in range(4):
@@ -201,16 +194,12 @@ def tile_layernormgrucell_pb_kernel(tc, x, h, r, z, W_in, b_in, W_hn, b_hn, out)
             nc.vector.tensor_tensor(out=kap[:, lo:hi], in0=rho[:, NT + lo:NT + hi], in1=std[:, lo:hi], op=ALU.mult)
             nc.vector.tensor_tensor(out=nb[:, lo:hi], in0=nmu[:, lo:hi], in1=rho[:, lo:hi], op=ALU.mult)
 
-        warm(W0)
-        spread_biases()
         t_weight(0, 0)
-        warm(W1)
+        spread_biases()
         q_weight(0, 0)
         t_weight(0, 1)
-        warm(W2)
         t_rows(0, 0)
         t_rows(0, 1)
-        warm(W3)
         q_weight(0, 1)
         q_rows(0, 0)
         q_rows(0, 1)

@@ -59,27 +59,25 @@ def tile_layernormgrucell_pb_kernel(tc, x, h, r, z, W_in, b_in, W_hn, b_hn, out)
 
         out_v = out.rearrange("(p t) k -> p t k", t=NT)
 
-        def load_pairs(view, tag, resident):
-            tiles = []
-            for i in range(NT // 2):
-                if resident:
-                    t_ = keep.tile([P, 2 * N], BF16, name="%s%d" % (tag, i))
-                else:
-                    t_ = rawp.tile([P, 2 * N], BF16, name="%s%d" % (tag, i), tag=tag[0:2])
-                nc.sync.dma_start(out=t_[:].rearrange("p (c k) -> p c k", c=2),
-                                  in_=view[:, 2 * i:2 * i + 2, :])
-                tiles.append(t_)
-                if tag == "wwin" and i == 1:
-                    nc.sync.dma_start(out=zb[0:1, 0:N], in_=b_in.rearrange("(o n) -> o n", o=1))
-                    nc.sync.dma_start(out=zb[0:1, N:2 * N], in_=b_hn.rearrange("(o n) -> o n", o=1))
-            return tiles
+        def load_pair(view, i, tag, resident):
+            if resident:
+                t_ = keep.tile([P, 2 * N], BF16, name="%s%d" % (tag, i))
+            else:
+                t_ = rawp.tile([P, 2 * N], BF16, name="%s%d" % (tag, i), tag=tag[0:2])
+            nc.sync.dma_start(out=t_[:].rearrange("p (c k) -> p c k", c=2), in_=view[:, 2 * i:2 * i + 2, :])
+            return t_
 
-        win_raw = load_pairs(W_in.rearrange("(c p) k -> p c k", p=P), "wwin", False)
-        x_raw = load_pairs(x.rearrange("(p t) k -> p t k", t=NT), "xrx", False)
-        h_raw = load_pairs(h.rearrange("(p t) k -> p t k", t=NT), "hraw", True)
-        z_raw = load_pairs(z.rearrange("(p t) k -> p t k", t=NT), "zraw", True)
-        whn_raw = load_pairs(W_hn.rearrange("(c p) k -> p c k", p=P), "wwhn", False)
-        r_raw = load_pairs(r.rearrange("(p t) k -> p t k", t=NT), "xrr", False)
+        views = {"wwin": W_in.rearrange("(c p) k -> p c k", p=P), "wwhn": W_hn.rearrange("(c p) k -> p c k", p=P),
+                 "xrx": x.rearrange("(p t) k -> p t k", t=NT), "hraw": h.rearrange("(p t) k -> p t k", t=NT),
+                 "zraw": z.rearrange("(p t) k -> p t k", t=NT), "xrr": r.rearrange("(p t) k -> p t k", t=NT)}
+        raws = {}
+        for tag, i in (("wwin", 0), ("wwin", 1), ("bias", 0), ("wwin", 2), ("wwin", 3), ("xrx", 0), ("xrx", 1), ("xrx", 2), ("xrx", 3), ("hraw", 0), ("hraw", 1), ("hraw", 2), ("hraw", 3), ("zraw", 0), ("zraw", 1), ("wwhn", 0), ("wwhn", 1), ("wwhn", 2), ("wwhn", 3), ("zraw", 2), ("zraw", 3), ("xrr", 0), ("xrr", 1), ("xrr", 2), ("xrr", 3)):
+            if tag == "bias":
+                nc.sync.dma_start(out=zb[0:1, 0:N], in_=b_in.rearrange("(o n) -> o n", o=1))
+                nc.sync.dma_start(out=zb[0:1, N:2 * N], in_=b_hn.rearrange("(o n) -> o n", o=1))
+            else:
+                raws.setdefault(tag, []).append(load_pair(views[tag], i, tag, tag in ("hraw", "zraw")))
+        win_raw, x_raw, h_raw, z_raw, whn_raw, r_raw = (raws[k] for k in ("wwin", "xrx", "hraw", "zraw", "wwhn", "xrr"))
         w_raw = (win_raw, whn_raw)
         row_raw = (x_raw, h_raw)
 
@@ -222,8 +220,7 @@ def tile_layernormgrucell_pb_kernel(tc, x, h, r, z, W_in, b_in, W_hn, b_hn, out)
 
         product(0, 4)
         product(0, 5)
-        t_rows(1, 2)
-        t_rows(1, 3)
+        t_weight(1, 0)
         add_bias(0, 4)
         add_bias(0, 5)
         q_rows(1, 0)
@@ -231,13 +228,12 @@ def tile_layernormgrucell_pb_kernel(tc, x, h, r, z, W_in, b_in, W_hn, b_hn, out)
 
         product(0, 6)
         product(0, 7)
-        t_weight(1, 0)
-        add_bias(0, 6)
-        q_rows(1, 2)
-        q_rows(1, 3)
         t_weight(1, 1)
+        add_bias(0, 6)
         add_bias(0, 7)
         q_weight(1, 0)
+        t_rows(1, 2)
+        t_rows(1, 3)
         q_weight(1, 1)
 
         product(1, 0)
@@ -247,6 +243,9 @@ def tile_layernormgrucell_pb_kernel(tc, x, h, r, z, W_in, b_in, W_hn, b_hn, out)
             squares_of(0, t)
         for t in range(NT):
             add_bias(1, t)
+            if t == 0:
+                q_rows(1, 2)
+                q_rows(1, 3)
             if t + 2 < NT:
                 product(1, t + 2)
             mean_of(1, t)

@@ -34,12 +34,12 @@ def tile_layernormgrucell_pb_kernel(tc, x, h, r, z, W_in, b_in, W_hn, b_hn, out)
         tpp = ctx.enter_context(tc.psum_pool(name="tp", bufs=4))
         mxp = ctx.enter_context(tc.psum_pool(name="mx", bufs=4))
 
+        ones = const.tile([P, HALF], BF16, name="ones")
+        nc.vector.memset(ones[:], 1.0)
         zb = const.tile([P, 2 * N], BF16, name="zb")
         nc.vector.memset(zb[:].bitcast(I32), 0)
         ident = const.tile([P, P], F32, name="ident")
         make_identity(nc, ident[:])
-        ones = const.tile([P, P], BF16, name="ones")
-        nc.vector.memset(ones[:], 1.0)
         ident_bf = const.tile([P, P], BF16, name="ident_bf")
         make_identity(nc, ident_bf[:])
         eps_t = const.tile([P, 1], F32, name="eps_t")
@@ -106,10 +106,15 @@ def tile_layernormgrucell_pb_kernel(tc, x, h, r, z, W_in, b_in, W_hn, b_hn, out)
         grouped = {}
         banks = {}
 
+        def warm(n):
+            ps = mxp.tile([P, HALF], F32, name="ps", tag="mx")
+            for i in range(n):
+                nc.tensor.matmul(out=ps[:], lhsT=ones[:, 0:P], rhs=ones[:], start=True, stop=True)
+
         def spread_biases():
             for k in range(4):
                 ps = mxp.tile([P, HALF], F32, name="ps", tag="mx")
-                nc.tensor.matmul(out=ps[:], lhsT=ones[:], rhs=zb[:, k * HALF:(k + 1) * HALF],
+                nc.tensor.matmul(out=ps[:], lhsT=ones[:, 0:P], rhs=zb[:, k * HALF:(k + 1) * HALF],
                                  start=True, stop=True)
                 if k < 2:
                     nc.vector.tensor_copy(out=bias[:, k * HALF:(k + 1) * HALF], in_=ps[:])
@@ -192,6 +197,7 @@ def tile_layernormgrucell_pb_kernel(tc, x, h, r, z, W_in, b_in, W_hn, b_hn, out)
             nc.vector.tensor_tensor(out=kap[:, lo:hi], in0=rho[:, NT + lo:NT + hi], in1=std[:, lo:hi], op=ALU.mult)
             nc.vector.tensor_tensor(out=nb[:, lo:hi], in0=nmu[:, lo:hi], in1=rho[:, lo:hi], op=ALU.mult)
 
+        warm(5)
         t_weight(0, 0)
         spread_biases()
         q_weight(0, 0)
@@ -199,23 +205,23 @@ def tile_layernormgrucell_pb_kernel(tc, x, h, r, z, W_in, b_in, W_hn, b_hn, out)
         t_rows(0, 0)
         t_rows(0, 1)
         q_weight(0, 1)
+        t_rows(0, 2)
         q_rows(0, 0)
         q_rows(0, 1)
 
         product(0, 0)
         product(0, 1)
-        t_rows(0, 2)
         t_rows(0, 3)
+        t_rows(1, 0)
         add_bias(0, 0)
         add_bias(0, 1)
+        q_rows(0, 2)
 
         product(0, 2)
         product(0, 3)
-        t_rows(1, 0)
         t_rows(1, 1)
         add_bias(0, 2)
         add_bias(0, 3)
-        q_rows(0, 2)
         q_rows(0, 3)
 
         product(0, 4)

@@ -18,8 +18,9 @@ NT = N // P
 HALF = 512
 EPS = 1e-5
 FLOPS = 2 * 2 * N * N * N
-BATCHES = ((0, 1, 2, 3), (4, 5, 6, 7))
-G_LAST = (0, 1, 4)
+BATCHES = ((0, 1, 2, 3, 4, 5, 6, 7),)
+FIRST, SECOND = (0, 1, 2, 3), (4, 5, 6, 7)
+G_LAST = (0, 1, 2)
 V_CHUNKS = (0, 2, 4, 6)
 
 
@@ -188,12 +189,15 @@ def tile_layernormgrucell_pb_kernel(tc, x, h, r, z, W_in, b_in, W_hn, b_hn, out)
             nc.scalar.activation(out=junk[:], in_=acc[m][t][:], func=ACT.Square, bias=nmu[:, i:i + 1],
                                  scale=1.0, accum_out=ssq[:, i:i + 1])
 
+        def both(ap, lo, hi):
+            return ap.rearrange("p (m t) -> p m t", m=2)[:, :, lo:hi]
+
+        def roots(lo, hi):
+            nc.scalar.activation(out=both(std[:], lo, hi), in_=both(ssq[:], lo, hi), func=ACT.Sqrt, bias=eps_t[:],
+                                 scale=1.0 / N)
+
         def row_scales(lo, hi):
-            def both(ap):
-                return ap.rearrange("p (m t) -> p m t", m=2)[:, :, lo:hi]
-            nc.scalar.activation(out=both(std[:]), in_=both(ssq[:]), func=ACT.Sqrt, bias=eps_t[:], scale=1.0 / N)
-            nc.scalar.activation(out=scr[:, 0:1], in_=eps_t[:], func=ACT.Tanh)
-            nc.vector.reciprocal(out=both(rho[:]), in_=both(std[:]))
+            nc.vector.reciprocal(out=both(rho[:], lo, hi), in_=both(std[:], lo, hi))
             nc.vector.tensor_tensor(out=kap[:, lo:hi], in0=rho[:, NT + lo:NT + hi], in1=std[:, lo:hi], op=ALU.mult)
             nc.vector.tensor_tensor(out=nb[:, lo:hi], in0=nmu[:, lo:hi], in1=rho[:, lo:hi], op=ALU.mult)
 
@@ -244,7 +248,7 @@ def tile_layernormgrucell_pb_kernel(tc, x, h, r, z, W_in, b_in, W_hn, b_hn, out)
 
         product(1, 0)
         product(1, 1)
-        for t in BATCHES[0]:
+        for t in FIRST:
             mean_of(0, t)
             squares_of(0, t)
         for t in range(NT):
@@ -255,19 +259,27 @@ def tile_layernormgrucell_pb_kernel(tc, x, h, r, z, W_in, b_in, W_hn, b_hn, out)
             if t + 2 < NT:
                 product(1, t + 2)
             mean_of(1, t)
-            if t in BATCHES[0]:
+            if t in FIRST:
                 squares_of(1, t)
+        roots(FIRST[0], FIRST[-1] + 1)
+        for t in SECOND:
+            squares_of(1, t)
+        for t in SECOND:
+            mean_of(0, t)
+            squares_of(0, t)
+        roots(SECOND[0], SECOND[-1] + 1)
+        nc.scalar.activation(out=scr[:, 0:1], in_=eps_t[:], func=ACT.Tanh)
 
         for b in range(len(BATCHES)):
             tiles = BATCHES[b]
             for t in tiles:
                 nc.vector.scalar_tensor_tensor(out=c_t[t][:], in0=c_t[t][:], scalar=nmu[:, NT + t:NT + t + 1],
                                                in1=tile_of(r_raw, t), op0=ALU.add, op1=ALU.mult)
-            row_scales(tiles[0], tiles[-1] + 1)
-            if b + 1 < len(BATCHES):
-                for t in BATCHES[b + 1]:
-                    squares_of(1, t)
             for t in tiles:
+                if t == FIRST[0]:
+                    row_scales(FIRST[0], FIRST[-1] + 1)
+                if t == SECOND[0]:
+                    row_scales(SECOND[0], SECOND[-1] + 1)
                 nc.vector.scalar_tensor_tensor(out=a_t[t][:], in0=c_t[t][:], scalar=kap[:, t:t + 1],
                                                in1=a_t[t][:], op0=ALU.mult, op1=ALU.add)
                 nc.scalar.activation(out=a_t[t][:], in_=a_t[t][:], func=ACT.Tanh,
@@ -277,20 +289,18 @@ def tile_layernormgrucell_pb_kernel(tc, x, h, r, z, W_in, b_in, W_hn, b_hn, out)
                     mean_of(0, t)
                     squares_of(0, t)
             for t in tiles:
+                if t % 2 == 0:
+                    zp = mxp.tile([P, N], BF16, name="zp", tag="mx")
+                else:
+                    zp = tpp.tile([P, N], BF16, name="zq", tag="tp")
+                banks[("z", t)] = zp
                 for i in range(2):
                     cols = slice(i * HALF, (i + 1) * HALF)
-                    if t % 2 == 0:
-                        zp = mxp.tile([P, HALF], F32, name="zp", tag="mx")
-                    else:
-                        zp = tpp.tile([P, HALF], F32, name="zq", tag="tp")
-                    banks[("z", t, i)] = zp
-                    nc.tensor.matmul(out=zp[:], lhsT=ident_bf[:], rhs=tile_of(z_raw, t)[:, cols],
+                    nc.tensor.matmul(out=zp[:, cols], lhsT=ident_bf[:], rhs=tile_of(z_raw, t)[:, cols],
                                      start=True, stop=True)
             for t in tiles:
-                for i in range(2):
-                    cols = slice(i * HALF, (i + 1) * HALF)
-                    nc.vector.scalar_tensor_tensor(out=a_t[t][:, cols], in0=banks[("z", t, i)][:], scalar=1.0,
-                                                   in1=a_t[t][:, cols], op0=ALU.subtract, op1=ALU.mult)
+                nc.vector.scalar_tensor_tensor(out=a_t[t][:], in0=banks[("z", t)][:], scalar=1.0,
+                                               in1=a_t[t][:], op0=ALU.subtract, op1=ALU.mult)
             for t in tiles:
                 if t in G_LAST:
                     for i in range(2):

@@ -134,13 +134,18 @@ def tile_layernormgrucell_pb_kernel(tc, x, h, r, z, W_in, b_in, W_hn, b_hn, out)
             else:
                 nc.scalar.copy(out=dst, in_=src)
 
-        def t_weight(m, half):
-            gw = grp.tile([P, 4 * N], BF16, name="gw", tag="gw", align_bytes=64)
-            grouped[("w", m, half)] = gw
+        def t_weight_half(m, half, part):
+            if part == 0:
+                grouped[("w", m, half)] = grp.tile([P, 4 * N], BF16, name="gw", tag="gw", align_bytes=64)
+            gw = grouped[("w", m, half)]
             gview = gw[:].bitcast(F32).rearrange("p (g c r u) -> p g c r u", g=2, c=4, u=2)
-            for c4 in range(4):
+            for c4 in (2 * part, 2 * part + 1):
                 c = 4 * half + c4
                 transpose_out(w_raw[m][c // 2], c % 2, m == 0 and c in V_CHUNKS, gview[:, :, c4, :, :])
+
+        def t_weight(m, half):
+            t_weight_half(m, half, 0)
+            t_weight_half(m, half, 1)
 
         def q_weight(m, half):
             cols = slice(half * N, (half + 1) * N)
@@ -214,31 +219,33 @@ def tile_layernormgrucell_pb_kernel(tc, x, h, r, z, W_in, b_in, W_hn, b_hn, out)
         q_rows(0, 1)
 
         product(0, 0)
-        product(0, 1)
         t_rows(0, 3)
+        product(0, 1)
         t_rows(1, 0)
         add_bias(0, 0)
         add_bias(0, 1)
         q_rows(0, 2)
 
         product(0, 2)
-        product(0, 3)
         t_rows(1, 1)
+        product(0, 3)
         add_bias(0, 2)
         add_bias(0, 3)
         q_rows(0, 3)
 
         product(0, 4)
+        t_weight_half(1, 0, 0)
         product(0, 5)
-        t_weight(1, 0)
+        t_weight_half(1, 0, 1)
         add_bias(0, 4)
         add_bias(0, 5)
         q_rows(1, 0)
         q_rows(1, 1)
 
         product(0, 6)
+        t_weight_half(1, 1, 0)
         product(0, 7)
-        t_weight(1, 1)
+        t_weight_half(1, 1, 1)
         add_bias(0, 6)
         add_bias(0, 7)
         q_weight(1, 0)

from contextlib import ExitStack

import concourse.mybir as mybir
from concourse.masks import make_identity

F32 = mybir.dt.float32
BF16 = mybir.dt.bfloat16
U32 = mybir.dt.uint32
U8 = mybir.dt.uint8
I32 = mybir.dt.int32
FP8X4 = mybir.dt.float8_e4m3fn_x4
ALU = mybir.AluOpType
ACT = mybir.ActivationFunctionType

P = 128
N = 1024
NT = N // P
HALF = 512
EPS = 1e-5
FLOPS = 2 * 2 * N * N * N
BATCHES = ((0, 1, 2, 3, 4, 5, 6, 7),)
FIRST, SECOND = (0, 1, 2, 3), (4, 5, 6, 7)
G_LAST = (0, 1, 2)
V_CHUNKS = (0, 2, 4, 6)


def tile_layernormgrucell_pb_kernel(tc, x, h, r, z, W_in, b_in, W_hn, b_hn, out):
    nc = tc.nc
    with ExitStack() as ctx:
        ctx.enter_context(tc.manual_schedule())
        const = ctx.enter_context(tc.tile_pool(name="const", bufs=1))
        rawp = ctx.enter_context(tc.tile_pool(name="raw", bufs=4))
        grp = ctx.enter_context(tc.tile_pool(name="grouped", bufs=2))
        keep = ctx.enter_context(tc.tile_pool(name="keep", bufs=1))
        tpp = ctx.enter_context(tc.psum_pool(name="tp", bufs=4))
        mxp = ctx.enter_context(tc.psum_pool(name="mx", bufs=4))

        ones = const.tile([P, HALF], BF16, name="ones")
        nc.vector.memset(ones[:], 1.0)
        zb = const.tile([P, 2 * N], BF16, name="zb")
        nc.vector.memset(zb[:].bitcast(I32), 0)
        ident = const.tile([P, P], F32, name="ident")
        make_identity(nc, ident[:])
        ident_bf = const.tile([P, P], BF16, name="ident_bf")
        make_identity(nc, ident_bf[:])
        eps_t = const.tile([P, 1], F32, name="eps_t")
        nc.vector.memset(eps_t[:], EPS)
        scr = const.tile([P, 2], F32, name="scr")
        nc.scalar.activation(out=scr[:, 0:1], in_=eps_t[:], func=ACT.Sqrt)

        bias = const.tile([P, 2 * N], F32, name="bias")
        sums = const.tile([P, 4 * NT], F32, name="sums")
        nmu = const.tile([P, 2 * NT], F32, name="nmu")
        ssq = const.tile([P, 2 * NT], F32, name="ssq")
        std = const.tile([P, 2 * NT], F32, name="std")
        rho = const.tile([P, 2 * NT], F32, name="rho")
        kap = const.tile([P, NT], F32, name="kap")
        nb = const.tile([P, NT], F32, name="nb")
        junk = const.tile([P, N], BF16, name="junk")

        out_v = out.rearrange("(p t) k -> p t k", t=NT)

        def load_pair(view, i, tag, resident):
            if resident:
                t_ = keep.tile([P, 2 * N], BF16, name="%s%d" % (tag, i))
            else:
                t_ = rawp.tile([P, 2 * N], BF16, name="%s%d" % (tag, i), tag=tag[0:2])
            nc.sync.dma_start(out=t_[:].rearrange("p (c k) -> p c k", c=2), in_=view[:, 2 * i:2 * i + 2, :])
            return t_

        views = {"wwin": W_in.rearrange("(c p) k -> p c k", p=P), "wwhn": W_hn.rearrange("(c p) k -> p c k", p=P),
                 "xrx": x.rearrange("(p t) k -> p t k", t=NT), "hraw": h.rearrange("(p t) k -> p t k", t=NT),
                 "zraw": z.rearrange("(p t) k -> p t k", t=NT), "xrr": r.rearrange("(p t) k -> p t k", t=NT)}
        raws = {}
        for tag, i in (("wwin", 0), ("wwin", 1), ("bias", 0), ("wwin", 2), ("wwin", 3), ("xrx", 0), ("xrx", 1), ("xrx", 2), ("xrx", 3), ("hraw", 0), ("hraw", 1), ("hraw", 2), ("hraw", 3), ("zraw", 0), ("zraw", 1), ("wwhn", 0), ("wwhn", 1), ("wwhn", 2), ("wwhn", 3), ("zraw", 2), ("zraw", 3), ("xrr", 0), ("xrr", 1), ("xrr", 2), ("xrr", 3)):
            if tag == "bias":
                nc.sync.dma_start(out=zb[0:1, 0:N], in_=b_in.rearrange("(o n) -> o n", o=1))
                nc.sync.dma_start(out=zb[0:1, N:2 * N], in_=b_hn.rearrange("(o n) -> o n", o=1))
            else:
                raws.setdefault(tag, []).append(load_pair(views[tag], i, tag, tag in ("hraw", "zraw")))
        win_raw, x_raw, h_raw, z_raw, whn_raw, r_raw = (raws[k] for k in ("wwin", "xrx", "hraw", "zraw", "wwhn", "xrr"))
        w_raw = (win_raw, whn_raw)
        row_raw = (x_raw, h_raw)

        def tile_of(raw, t):
            return raw[t // 2][:, (t % 2) * N:(t % 2 + 1) * N]

        zh_t = []
        for t in range(NT):
            if t < NT // 2:
                zh = keep.tile([P, N], F32, name="zh%d" % t)
            else:
                zh = rawp.tile([P, N], F32, name="zh%d" % t, tag="ww")
            for i in range(2):
                cols = slice(i * HALF, (i + 1) * HALF)
                nc.gpsimd.tensor_tensor(out=zh[:, cols], in0=tile_of(z_raw, t)[:, cols],
                                        in1=tile_of(h_raw, t)[:, cols], op=ALU.mult)
            zh_t.append(zh)

        acc = ([keep.tile([P, N], F32, name="a%d" % t) for t in range(NT)],
               [keep.tile([P, N], F32, name="c%d" % t) for t in range(NT)])
        a_t, c_t = acc
        w_codes = [keep.tile([P, 2 * N], U32, name="cw%d" % m, align_bytes=64) for m in range(2)]
        w_scales = [keep.tile([P, 2 * N], U8, name="sw%d" % m, align_bytes=64) for m in range(2)]
        r_codes = [keep.tile([P, 2 * N], U32, name="cr%d" % m, align_bytes=64) for m in range(2)]
        r_scales = [keep.tile([P, 2 * N], U8, name="sr%d" % m, align_bytes=64) for m in range(2)]
        grouped = {}
        banks = {}

        def warm(n):
            ps = mxp.tile([P, HALF], F32, name="ps", tag="mx")
            for i in range(n):
                nc.tensor.matmul(out=ps[:], lhsT=ones[:, 0:P], rhs=ones[:], start=True, stop=True)

        def spread_biases():
            for k in range(4):
                ps = mxp.tile([P, HALF], F32, name="ps", tag="mx")
                nc.tensor.matmul(out=ps[:], lhsT=ones[:, 0:P], rhs=zb[:, k * HALF:(k + 1) * HALF],
                                 start=True, stop=True)
                if k < 2:
                    nc.vector.tensor_copy(out=bias[:, k * HALF:(k + 1) * HALF], in_=ps[:])
                else:
                    nc.scalar.copy(out=bias[:, k * HALF:(k + 1) * HALF], in_=ps[:])

        def transpose_out(raw_pair, cc, on_vector, dst):
            tp = tpp.tile([P, HALF], F32, name="tp", tag="tp")
            words = raw_pair[:].bitcast(F32)
            for q in range(4):
                nc.tensor.transpose(tp[:, q * P:(q + 1) * P],
                                    words[:, cc * HALF + q * P:cc * HALF + (q + 1) * P], ident[:])
            src = tp[:].rearrange("p (g u r) -> p g r u", g=2, u=2)
            if on_vector:
                nc.vector.tensor_copy(out=dst, in_=src)
            else:
                nc.scalar.copy(out=dst, in_=src)

        def t_weight_half(m, half, part):
            if part == 0:
                grouped[("w", m, half)] = grp.tile([P, 4 * N], BF16, name="gw", tag="gw", align_bytes=64)
            gw = grouped[("w", m, half)]
            gview = gw[:].bitcast(F32).rearrange("p (g c r u) -> p g c r u", g=2, c=4, u=2)
            for c4 in (2 * part, 2 * part + 1):
                c = 4 * half + c4
                transpose_out(w_raw[m][c // 2], c % 2, m == 0 and c in V_CHUNKS, gview[:, :, c4, :, :])

        def t_weight(m, half):
            t_weight_half(m, half, 0)
            t_weight_half(m, half, 1)

        def q_weight(m, half):
            cols = slice(half * N, (half + 1) * N)
            nc.vector.quantize_mx(out=w_codes[m][:, cols].bitcast(FP8X4), scales=w_scales[m][:, cols],
                                  in_=grouped[("w", m, half)][:])

        def t_rows(m, pair):
            gx = grp.tile([P, 2 * N], BF16, name="gx", tag="gx", bufs=3, align_bytes=64)
            grouped[("r", m, pair)] = gx
            gview = gx[:].bitcast(F32).rearrange("p (t g r u) -> p t g r u", t=2, g=2, u=2)
            for cc in range(2):
                transpose_out(row_raw[m][pair], cc, False, gview[:, cc, :, :, :])

        def q_rows(m, pair):
            cols = slice(pair * 4 * P, (pair + 1) * 4 * P)
            nc.vector.quantize_mx(out=r_codes[m][:, cols].bitcast(FP8X4), scales=r_scales[m][:, cols],
                                  in_=grouped[("r", m, pair)][:])

        def product(m, t):
            for half in range(2):
                ps = mxp.tile([P, HALF], F32, name="ps", tag="mx")
                banks[(m, t, half)] = ps
                for g in range(2):
                    lcols = slice(t * 2 * P + g * P, t * 2 * P + (g + 1) * P)
                    rcols = slice(half * N + g * HALF, half * N + (g + 1) * HALF)
                    nc.tensor.matmul_mx(out=ps[:], lhsT=r_codes[m][:, lcols].bitcast(FP8X4),
                                        lhsT_scale=r_scales[m][:, lcols],
                                        rhs=w_codes[m][:, rcols].bitcast(FP8X4), rhs_scale=w_scales[m][:, rcols],
                                        start=(g == 0), stop=(g == 1))

        def add_bias(m, t):
            for half in range(2):
                k = (m * NT + t) * 2 + half
                nc.vector.scalar_tensor_tensor(
                    out=acc[m][t][:, half * HALF:(half + 1) * HALF], in0=banks[(m, t, half)][:], scalar=1.0,
                    in1=bias[:, m * N + half * HALF:m * N + (half + 1) * HALF],
                    op0=ALU.mult, op1=ALU.add, accum_out=sums[:, k:k + 1])

        def mean_of(m, t):
            i = m * NT + t
            nc.scalar.activation(out=scr[:, 0:2], in_=sums[:, 2 * i:2 * i + 2], func=ACT.Identity,
                                 scale=-1.0 / N, accum_out=nmu[:, i:i + 1])

        def squares_of(m, t):
            i = m * NT + t
            nc.scalar.activation(out=junk[:], in_=acc[m][t][:], func=ACT.Square, bias=nmu[:, i:i + 1],
                                 scale=1.0, accum_out=ssq[:, i:i + 1])

        def both(ap, lo, hi):
            return ap.rearrange("p (m t) -> p m t", m=2)[:, :, lo:hi]

        def roots(lo, hi):
            nc.scalar.activation(out=both(std[:], lo, hi), in_=both(ssq[:], lo, hi), func=ACT.Sqrt, bias=eps_t[:],
                                 scale=1.0 / N)

        def row_scales(lo, hi):
            nc.vector.reciprocal(out=both(rho[:], lo, hi), in_=both(std[:], lo, hi))
            nc.vector.tensor_tensor(out=kap[:, lo:hi], in0=rho[:, NT + lo:NT + hi], in1=std[:, lo:hi], op=ALU.mult)
            nc.vector.tensor_tensor(out=nb[:, lo:hi], in0=nmu[:, lo:hi], in1=rho[:, lo:hi], op=ALU.mult)

        warm(5)
        t_weight(0, 0)
        spread_biases()
        q_weight(0, 0)
        t_weight(0, 1)
        t_rows(0, 0)
        t_rows(0, 1)
        q_weight(0, 1)
        t_rows(0, 2)
        q_rows(0, 0)
        q_rows(0, 1)

        product(0, 0)
        t_rows(0, 3)
        product(0, 1)
        t_rows(1, 0)
        add_bias(0, 0)
        add_bias(0, 1)
        q_rows(0, 2)

        product(0, 2)
        t_rows(1, 1)
        product(0, 3)
        add_bias(0, 2)
        add_bias(0, 3)
        q_rows(0, 3)

        product(0, 4)
        t_weight_half(1, 0, 0)
        product(0, 5)
        t_weight_half(1, 0, 1)
        add_bias(0, 4)
        add_bias(0, 5)
        q_rows(1, 0)
        q_rows(1, 1)

        product(0, 6)
        t_weight_half(1, 1, 0)
        product(0, 7)
        t_weight_half(1, 1, 1)
        add_bias(0, 6)
        add_bias(0, 7)
        q_weight(1, 0)
        t_rows(1, 2)
        t_rows(1, 3)
        q_weight(1, 1)

        product(1, 0)
        product(1, 1)
        for t in FIRST:
            mean_of(0, t)
            squares_of(0, t)
        for t in range(NT):
            add_bias(1, t)
            if t == 0:
                q_rows(1, 2)
                q_rows(1, 3)
            if t + 2 < NT:
                product(1, t + 2)
            mean_of(1, t)
            if t in FIRST:
                squares_of(1, t)
        roots(FIRST[0], FIRST[-1] + 1)
        for t in SECOND:
            squares_of(1, t)
        for t in SECOND:
            mean_of(0, t)
            squares_of(0, t)
        roots(SECOND[0], SECOND[-1] + 1)
        nc.scalar.activation(out=scr[:, 0:1], in_=eps_t[:], func=ACT.Tanh)

        for b in range(len(BATCHES)):
            tiles = BATCHES[b]
            for t in tiles:
                nc.vector.scalar_tensor_tensor(out=c_t[t][:], in0=c_t[t][:], scalar=nmu[:, NT + t:NT + t + 1],
                                               in1=tile_of(r_raw, t), op0=ALU.add, op1=ALU.mult)
            for t in tiles:
                if t == FIRST[0]:
                    row_scales(FIRST[0], FIRST[-1] + 1)
                if t == SECOND[0]:
                    row_scales(SECOND[0], SECOND[-1] + 1)
                nc.vector.scalar_tensor_tensor(out=a_t[t][:], in0=c_t[t][:], scalar=kap[:, t:t + 1],
                                               in1=a_t[t][:], op0=ALU.mult, op1=ALU.add)
                nc.scalar.activation(out=a_t[t][:], in_=a_t[t][:], func=ACT.Tanh,
                                     bias=nb[:, t:t + 1], scale=rho[:, t:t + 1])
            if b + 1 < len(BATCHES):
                for t in BATCHES[b + 1]:
                    mean_of(0, t)
                    squares_of(0, t)
            for t in tiles:
                if t % 2 == 0:
                    zp = mxp.tile([P, N], BF16, name="zp", tag="mx")
                else:
                    zp = tpp.tile([P, N], BF16, name="zq", tag="tp")
                banks[("z", t)] = zp
                for i in range(2):
                    cols = slice(i * HALF, (i + 1) * HALF)
                    nc.tensor.matmul(out=zp[:, cols], lhsT=ident_bf[:], rhs=tile_of(z_raw, t)[:, cols],
                                     start=True, stop=True)
            for t in tiles:
                nc.vector.scalar_tensor_tensor(out=a_t[t][:], in0=banks[("z", t)][:], scalar=1.0,
                                               in1=a_t[t][:], op0=ALU.subtract, op1=ALU.mult)
            for t in tiles:
                if t in G_LAST:
                    for i in range(2):
                        cols = slice(i * HALF, (i + 1) * HALF)
                        nc.gpsimd.tensor_tensor(out=a_t[t][:, cols], in0=zh_t[t][:, cols], in1=a_t[t][:, cols],
                                                op=ALU.subtract)
            if b + 1 == len(BATCHES):
                for t in tiles:
                    if t in G_LAST:
                        nc.sync.dma_start(out=out_v[:, t, :], in_=a_t[t][:])
            for t in tiles:
                if t not in G_LAST:
                    cuts = 2 if t == NT - 1 else 1
                    for i in range(cuts):
                        cols = slice(i * (N // cuts), (i + 1) * (N // cuts))
                        nc.vector.tensor_tensor(out=a_t[t][:, cols], in0=zh_t[t][:, cols], in1=a_t[t][:, cols],
                                                op=ALU.subtract)
                        nc.sync.dma_start(out=out_v[:, t, cols], in_=a_t[t][:, cols])
            if b + 1 < len(BATCHES):
                for t in tiles:
                    if t in G_LAST:
                        nc.sync.dma_start(out=out_v[:, t, :], in_=a_t[t][:])
